import numpy as np
import ml_dtypes


def mxq(x, axis, fmt="e4m3"):
    dtype, down = {"e4m3": (ml_dtypes.float8_e4m3fn, 7), "e5m2": (ml_dtypes.float8_e5m2, 14)}[fmt]
    v = np.moveaxis(np.asarray(x, np.float32).astype(ml_dtypes.bfloat16).astype(np.float64), axis, -1)
    blocks = v.reshape(v.shape[:-1] + (-1, 32))
    amax = np.abs(blocks).max(-1, keepdims=True)
    byte = np.maximum(np.where(amax > 0, np.frexp(amax)[1] - 1 + 127, 0) - down, 1)
    scale = np.exp2(byte - 127.0)
    codes = (blocks / scale).astype(np.float32).astype(dtype).astype(np.float64)
    return np.moveaxis((codes * scale).reshape(v.shape), -1, axis)


WIDE = False


def mx_kscale(k):
    if not WIDE:
        return np.ones(k)
    levels = np.array([10, -10, 5, -5, 0])
    a = np.random.permutation(np.resize(levels, k // 512 * 4)).reshape(k // 512, 4)
    idx = np.arange(k)
    return np.exp2(a[idx // 512, idx % 128 // 32])


BF16 = ml_dtypes.bfloat16


def bf(x):
    return np.asarray(x, np.float32).astype(BF16)


def f64(x):
    return np.asarray(x).astype(np.float64)


E2M1 = np.array([0.0, 0.5, 1.0, 1.5, 2.0, 3.0, 4.0, 6.0, -0.0, -0.5, -1.0, -1.5, -2.0, -3.0, -4.0, -6.0])


def pack_weight(w, fmt):
    k, n = w.shape
    w = f64(bf(w)).reshape(k // 32, 32, n)
    amax = np.abs(w).max(1)
    if fmt == "e4m3":
        byte = np.frexp(amax)[1] - 1 + 127 - 7
    else:
        mant, ex = np.frexp(amax / 6.0)
        byte = np.where(mant > 0.5, ex, ex - 1) + 127
    byte = np.clip(np.where(amax > 0, byte, 1), 1, 254)
    scaled = (w * np.exp2(127.0 - byte)[:, None, :]).reshape(k, n).astype(np.float32)
    by_word = np.ascontiguousarray(scaled.reshape(k // 512, 128, 4, n).transpose(0, 1, 3, 2))
    if fmt == "e4m3":
        words = by_word.astype(ml_dtypes.float8_e4m3fn).view(np.uint8)
    else:
        c = by_word.astype(ml_dtypes.float4_e2m1fn).view(np.uint8) & 0xF
        words = c[..., 0::2] | (c[..., 1::2] << 4)
    return np.ascontiguousarray(words), np.ascontiguousarray(byte.astype(np.uint8).reshape(k // 512, 16, n))


def unpack_weight(words, scales, fmt):
    g, p, n, _ = words.shape
    if fmt == "e4m3":
        vals = np.ascontiguousarray(words).view(ml_dtypes.float8_e4m3fn).astype(np.float64)
    else:
        nib = np.empty((g, p, n, 4), np.uint8)
        nib[..., 0::2] = words & 0xF
        nib[..., 1::2] = words >> 4
        vals = E2M1[nib]
    vals = vals * np.repeat(np.exp2(scales.astype(np.float64) - 127.0), 8, axis=1)[..., None]
    return vals.transpose(0, 1, 3, 2).reshape(g * 512, n)


B, D_IN, D_H, H_MX = 512, 1024, 1024, 1


def sigmoid(v):
    return 1.0 / (1.0 + np.exp(-v))


def setup_inputs():
    s = mx_kscale(D_IN)
    u = mx_kscale(D_H) if H_MX else np.ones(D_H)
    inp = {"x": bf(np.random.standard_normal((B, D_IN)) * s),
           "h": bf(np.random.standard_normal((B, D_H)) * u),
           "c": bf(np.random.standard_normal((B, D_H)))}
    for name in ["W_xi", "W_hi", "W_xf", "W_hf", "W_xo", "W_ho", "W_xc", "W_hc"]:
        rows, r = (D_IN, s) if name[2] == "x" else (D_H, u)
        words, scales = pack_weight(np.random.standard_normal((rows, D_H)) * 0.7 / np.sqrt(rows) / r[:, None], "e4m3")
        inp[name + "_words"] = words
        inp[name + "_scales"] = scales
    for name in ["b_i", "b_f", "b_o", "b_c"]:
        inp[name] = bf(np.random.standard_normal(D_H) * 0.3)
    return inp


def reference(x, h, c, W_xi_words, W_xi_scales, W_hi_words, W_hi_scales, W_xf_words, W_xf_scales, W_hf_words, W_hf_scales, W_xo_words, W_xo_scales, W_ho_words, W_ho_scales, W_xc_words, W_xc_scales, W_hc_words, W_hc_scales, b_i, b_f, b_o, b_c):
    Wx = np.concatenate([unpack_weight(W_xi_words, W_xi_scales, "e4m3"), unpack_weight(W_xf_words, W_xf_scales, "e4m3"), unpack_weight(W_xc_words, W_xc_scales, "e4m3"), unpack_weight(W_xo_words, W_xo_scales, "e4m3")], axis=1)
    Wh = np.concatenate([unpack_weight(W_hi_words, W_hi_scales, "e4m3"), unpack_weight(W_hf_words, W_hf_scales, "e4m3"), unpack_weight(W_hc_words, W_hc_scales, "e4m3"), unpack_weight(W_ho_words, W_ho_scales, "e4m3")], axis=1)
    b = np.concatenate([f64(b_i), f64(b_f), f64(b_c), f64(b_o)])
    gx = mxq(f64(x), 1, "e4m3") @ Wx
    if H_MX:
        gh = mxq(f64(h), 1, "e4m3") @ Wh
    else:
        gh = f64(h) @ Wh
    gates = gx + gh + b
    gi, gf, gc, go = np.split(gates, 4, axis=1)
    i = sigmoid(gi)
    f = sigmoid(gf)
    c_hat = np.tanh(gc)
    o = sigmoid(go)
    c_new = f * f64(c) + i * c_hat
    h_new = o * np.tanh(c_new)
    return (h_new, c_new)

@@ -1,0 +1,214 @@
+from contextlib import ExitStack
+
+import concourse.mybir as mybir
+from concourse.masks import make_identity
+
+F32 = mybir.dt.float32
+BF16 = mybir.dt.bfloat16
+I32 = mybir.dt.int32
+U32 = mybir.dt.uint32
+U8 = mybir.dt.uint8
+FP8X4 = mybir.dt.float8_e4m3fn_x4
+ACT = mybir.ActivationFunctionType
+ALU = mybir.AluOpType
+
+P = 128
+BATCH = 512
+FEATURES = 1024
+HIDDEN = 1024
+PACK = 4
+K_PASS = P * PACK
+K_GROUPS = FEATURES // K_PASS
+ROW_TILES = BATCH // P
+N_TILE = 512
+COL_HALVES = HIDDEN // N_TILE
+QUADRANTS = 4
+SOURCES = ("x", "h")
+GATES = ("i", "c", "f", "o")
+
+FLOPS = 2 * BATCH * (2 * FEATURES) * (4 * HIDDEN)
+
+
+def tile_lstmcell_kernel(
+    tc,
+    x, h, c,
+    W_xi_words, W_xi_scales, W_hi_words, W_hi_scales,
+    W_xf_words, W_xf_scales, W_hf_words, W_hf_scales,
+    W_xo_words, W_xo_scales, W_ho_words, W_ho_scales,
+    W_xc_words, W_xc_scales, W_hc_words, W_hc_scales,
+    b_i, b_f, b_o, b_c,
+    out_0, out_1,
+):
+    nc = tc.nc
+    activations = {"x": x, "h": h}
+    dram_words = {
+        ("i", "x"): W_xi_words, ("i", "h"): W_hi_words,
+        ("f", "x"): W_xf_words, ("f", "h"): W_hf_words,
+        ("o", "x"): W_xo_words, ("o", "h"): W_ho_words,
+        ("c", "x"): W_xc_words, ("c", "h"): W_hc_words,
+    }
+    dram_scales = {
+        ("i", "x"): W_xi_scales, ("i", "h"): W_hi_scales,
+        ("f", "x"): W_xf_scales, ("f", "h"): W_hf_scales,
+        ("o", "x"): W_xo_scales, ("o", "h"): W_ho_scales,
+        ("c", "x"): W_xc_scales, ("c", "h"): W_hc_scales,
+    }
+    dram_bias = {"i": b_i, "f": b_f, "o": b_o, "c": b_c}
+
+    with ExitStack() as stack:
+        keep = stack.enter_context(tc.tile_pool(name="keep", bufs=1))
+        work = stack.enter_context(tc.tile_pool(name="work", bufs=6))
+        psum = stack.enter_context(tc.psum_pool(name="psum", bufs=8))
+
+        raw = {}
+        grouped = {}
+        act_codes = {}
+        act_scales = {}
+        for src in SOURCES:
+            raw[src] = keep.tile([P, ROW_TILES, FEATURES], BF16, name="raw_" + src)
+            grouped[src] = keep.tile(
+                [P, ROW_TILES, K_GROUPS * P * PACK], BF16, name="grouped_" + src, align_bytes=64
+            )
+            act_codes[src] = keep.tile(
+                [P, ROW_TILES, K_GROUPS * P], U32, name="codes_" + src, align_bytes=64
+            )
+            act_scales[src] = keep.tile(
+                [P, ROW_TILES, K_GROUPS * P], U8, name="scales_" + src, align_bytes=64
+            )
+        w_words = {}
+        for gate in GATES:
+            for src in SOURCES:
+                w_words[(gate, src)] = keep.tile(
+                    [P, K_GROUPS, HIDDEN], U32, name="w_" + src + gate, align_bytes=64
+                )
+        w_planes = {}
+        for gate in GATES:
+            w_planes[gate] = keep.tile([P, HIDDEN], U8, name="planes_" + gate, align_bytes=64)
+        c_sb = keep.tile([P, ROW_TILES, HIDDEN], BF16)
+        bias_rows = keep.tile([P, len(GATES) * HIDDEN], BF16)
+        bias_all = keep.tile([P, len(GATES) * HIDDEN], F32)
+        ones = keep.tile([P, P], BF16)
+        identity = keep.tile([P, P], F32)
+        table_warm = keep.tile([P, 1], F32)
+
+        nc.vector.memset(table_warm[:], 0.0)
+        nc.scalar.activation(out=table_warm[:], in_=table_warm[:], func=ACT.Sigmoid)
+        nc.vector.memset(bias_rows[:], 0.0)
+        nc.vector.memset(ones[:], 1.0)
+        for gate in GATES:
+            nc.vector.memset(w_planes[gate][:].bitcast(I32), 0)
+        make_identity(nc, identity[:])
+
+        def load_scales(gate):
+            for s, src in enumerate(SOURCES):
+                for quad in range(QUADRANTS):
+                    first = 32 * quad + 4 * K_GROUPS * s
+                    nc.sync.dma_start(
+                        out=w_planes[gate][first : first + 4 * K_GROUPS, :].bitcast(I32),
+                        in_=dram_scales[(gate, src)][:, 4 * quad : 4 * quad + 4, :].bitcast(I32),
+                    )
+
+        def load_words(gate, half):
+            cols = slice(half * N_TILE, (half + 1) * N_TILE)
+            for src in SOURCES:
+                words = dram_words[(gate, src)].rearrange("g p n t -> p g (n t)").bitcast(I32)
+                nc.sync.dma_start(
+                    out=w_words[(gate, src)][:, :, cols].bitcast(I32), in_=words[:, :, cols]
+                )
+
+        for j, gate in enumerate(GATES):
+            nc.scalar.dma_start(
+                out=bias_rows[0:1, j * HIDDEN : (j + 1) * HIDDEN], in_=dram_bias[gate].unsqueeze(0)
+            )
+        for src in SOURCES:
+            for m in range(ROW_TILES):
+                nc.sync.dma_start(out=raw[src][:, m, :], in_=activations[src][m * P : (m + 1) * P, :])
+        for gate in GATES:
+            load_scales(gate)
+            load_words(gate, 0)
+            if gate == "c":
+                nc.sync.dma_start(out=c_sb[:], in_=c.rearrange("(m p) d -> p m d", p=P))
+        for gate in GATES:
+            load_words(gate, 1)
+
+        for j in range(len(GATES) * COL_HALVES):
+            cols = slice(j * N_TILE, (j + 1) * N_TILE)
+            spread = psum.tile([P, N_TILE], F32, tag="bank")
+            nc.tensor.matmul(out=spread[:], lhsT=ones[:], rhs=bias_rows[:, cols], start=True, stop=True)
+            nc.scalar.copy(out=bias_all[:, cols], in_=spread[:])
+
+        for src in SOURCES:
+            for m in range(ROW_TILES):
+                words = raw[src][:, m, :].bitcast(F32)
+                flipped = psum.tile([P, K_GROUPS * 2, P], F32, tag="bank")
+                for g in range(K_GROUPS):
+                    for u in range(2):
+                        first = g * (K_PASS // 2) + u
+                        nc.tensor.transpose(
+                            out=flipped[:, 2 * g + u, :],
+                            in_=words[:, first : (g + 1) * (K_PASS // 2) : 2],
+                            identity=identity[:],
+                        )
+                side_by_side = grouped[src][:, m, :].bitcast(F32).rearrange(
+                    "p (g b u) -> p g b u", g=K_GROUPS, u=2
+                )
+                permuted = flipped[:].rearrange("p (g u) b -> p g b u", u=2)
+                if m % 2 == 0:
+                    nc.vector.tensor_copy(out=side_by_side, in_=permuted)
+                else:
+                    nc.scalar.copy(out=side_by_side, in_=permuted)
+                nc.vector.quantize_mx(
+                    out=act_codes[src][:, m, :].bitcast(FP8X4),
+                    scales=act_scales[src][:, m, :],
+                    in_=grouped[src][:, m, :],
+                )
+
+        passes = [(s, src, g) for s, src in enumerate(SOURCES) for g in range(K_GROUPS)]
+        for half in range(COL_HALVES):
+            cols = slice(half * N_TILE, (half + 1) * N_TILE)
+            value = {}
+            for j, gate in enumerate(GATES):
+                for m in range(ROW_TILES):
+                    rows = slice(m * P, (m + 1) * P)
+                    acc = psum.tile([P, N_TILE], F32, tag="bank")
+                    for n, (s, src, g) in enumerate(passes):
+                        k_cols = slice(g * P, (g + 1) * P)
+                        plane_start = 4 * (K_GROUPS * s + g)
+                        nc.tensor.matmul_mx(
+                            out=acc[:],
+                            lhsT=act_codes[src][:, m, k_cols].bitcast(FP8X4),
+                            lhsT_scale=act_scales[src][:, m, k_cols],
+                            rhs=w_words[(gate, src)][:, g, cols].bitcast(FP8X4),
+                            rhs_scale=w_planes[gate][plane_start:P, cols],
+                            start=(n == 0),
+                            stop=(n == len(passes) - 1),
+                        )
+                    out_gate = work.tile([P, N_TILE], F32, name="gate_" + gate, tag="gate_" + gate)
+                    value[(gate, m)] = out_gate
+                    bias_cols = slice(j * HIDDEN + half * N_TILE, j * HIDDEN + (half + 1) * N_TILE)
+                    nc.vector.tensor_tensor(
+                        out=out_gate[:], in0=acc[:], in1=bias_all[:, bias_cols], op=ALU.add
+                    )
+                    nc.scalar.activation(
+                        out=out_gate[:], in_=out_gate[:], func=(ACT.Tanh if gate == "c" else ACT.Sigmoid)
+                    )
+                    if gate == "c":
+                        nc.gpsimd.tensor_tensor(
+                            out=out_gate[:], in0=value[("i", m)][:], in1=out_gate[:], op=ALU.mult
+                        )
+                    if gate == "f":
+                        nc.gpsimd.tensor_tensor(
+                            out=out_gate[:], in0=out_gate[:], in1=c_sb[:, m, cols], op=ALU.mult
+                        )
+                        nc.vector.tensor_tensor(
+                            out=out_gate[:], in0=out_gate[:], in1=value[("c", m)][:], op=ALU.add
+                        )
+                        nc.sync.dma_start(out=out_1[rows, cols], in_=out_gate[:])
+                        cell_tanh = work.tile([P, N_TILE], F32, tag="cell_tanh")
+                        value[("t", m)] = cell_tanh
+                        nc.scalar.activation(out=cell_tanh[:], in_=out_gate[:], func=ACT.Tanh)
+                    if gate == "o":
+                        nc.vector.tensor_tensor(
+                            out=out_gate[:], in0=out_gate[:], in1=value[("t", m)][:], op=ALU.mult
+                        )
+                        nc.sync.dma_start(out=out_0[rows, cols], in_=out_gate[:])

@@ -59,6 +59,7 @@ def tile_lstmcell_kernel(
         keep = stack.enter_context(tc.tile_pool(name="keep", bufs=1))
         work = stack.enter_context(tc.tile_pool(name="work", bufs=6))
         psum = stack.enter_context(tc.psum_pool(name="psum", bufs=8))
+        stack.enter_context(tc.manual_schedule())
 
         raw = {}
         grouped = {}
@@ -82,21 +83,25 @@ def tile_lstmcell_kernel(
                     [P, K_GROUPS, HIDDEN], U32, name="w_" + src + gate, align_bytes=64
                 )
         w_planes = {}
+        bias_rows = {}
+        bias_all = {}
         for gate in GATES:
             w_planes[gate] = keep.tile([P, HIDDEN], U8, name="planes_" + gate, align_bytes=64)
+            bias_rows[gate] = keep.tile([P, HIDDEN], BF16, name="bias_rows_" + gate)
+            bias_all[gate] = keep.tile([P, HIDDEN], BF16, name="bias_all_" + gate)
         c_sb = keep.tile([P, ROW_TILES, HIDDEN], BF16)
-        bias_rows = keep.tile([P, len(GATES) * HIDDEN], BF16)
-        bias_all = keep.tile([P, len(GATES) * HIDDEN], F32)
         ones = keep.tile([P, P], BF16)
         identity = keep.tile([P, P], F32)
         table_warm = keep.tile([P, 1], F32)
 
-        nc.vector.memset(table_warm[:], 0.0)
-        nc.scalar.activation(out=table_warm[:], in_=table_warm[:], func=ACT.Sigmoid)
-        nc.vector.memset(bias_rows[:], 0.0)
+        for gate in GATES:
+            nc.vector.memset(bias_rows[gate][:], 0.0)
+            nc.scalar.dma_start(out=bias_rows[gate][0:1, :], in_=dram_bias[gate].unsqueeze(0))
         nc.vector.memset(ones[:], 1.0)
         for gate in GATES:
             nc.vector.memset(w_planes[gate][:].bitcast(I32), 0)
+        nc.vector.memset(table_warm[:], 0.0)
+        nc.scalar.activation(out=table_warm[:], in_=table_warm[:], func=ACT.Sigmoid)
         make_identity(nc, identity[:])
 
         def load_scales(gate):
@@ -116,99 +121,121 @@ def tile_lstmcell_kernel(
                     out=w_words[(gate, src)][:, :, cols].bitcast(I32), in_=words[:, :, cols]
                 )
 
-        for j, gate in enumerate(GATES):
-            nc.scalar.dma_start(
-                out=bias_rows[0:1, j * HIDDEN : (j + 1) * HIDDEN], in_=dram_bias[gate].unsqueeze(0)
-            )
         for src in SOURCES:
-            for m in range(ROW_TILES):
-                nc.sync.dma_start(out=raw[src][:, m, :], in_=activations[src][m * P : (m + 1) * P, :])
+            by_tile = activations[src].rearrange("(m p) k -> p m k", p=P)
+            for first in range(0, ROW_TILES, 2):
+                nc.sync.dma_start(
+                    out=raw[src][:, first : first + 2, :], in_=by_tile[:, first : first + 2, :]
+                )
         for gate in GATES:
             load_scales(gate)
             load_words(gate, 0)
-            if gate == "c":
+            if gate == "f":
                 nc.sync.dma_start(out=c_sb[:], in_=c.rearrange("(m p) d -> p m d", p=P))
         for gate in GATES:
             load_words(gate, 1)
 
-        for j in range(len(GATES) * COL_HALVES):
-            cols = slice(j * N_TILE, (j + 1) * N_TILE)
-            spread = psum.tile([P, N_TILE], F32, tag="bank")
-            nc.tensor.matmul(out=spread[:], lhsT=ones[:], rhs=bias_rows[:, cols], start=True, stop=True)
-            nc.scalar.copy(out=bias_all[:, cols], in_=spread[:])
+        def transpose_and_regroup(src, m):
+            words = raw[src][:, m, :].bitcast(F32)
+            flipped = psum.tile([P, K_GROUPS * 2, P], F32, tag="bank")
+            for g in range(K_GROUPS):
+                for u in range(2):
+                    nc.tensor.transpose(
+                        out=flipped[:, 2 * g + u, :],
+                        in_=words[:, g * (K_PASS // 2) + u : (g + 1) * (K_PASS // 2) : 2],
+                        identity=identity[:],
+                    )
+            side_by_side = grouped[src][:, m, :].bitcast(F32).rearrange(
+                "p (g b u) -> p g b u", g=K_GROUPS, u=2
+            )
+            permuted = flipped[:].rearrange("p (g u) b -> p g b u", u=2)
+            if m % 2 == 0:
+                nc.vector.tensor_copy(out=side_by_side, in_=permuted)
+            else:
+                nc.scalar.copy(out=side_by_side, in_=permuted)
 
-        for src in SOURCES:
+        def quantise(src, m):
+            nc.vector.quantize_mx(
+                out=act_codes[src][:, m, :].bitcast(FP8X4),
+                scales=act_scales[src][:, m, :],
+                in_=grouped[src][:, m, :],
+            )
+
+        def spread_bias(gate):
+            spread = psum.tile([P, HIDDEN], BF16, tag="bank")
+            for half in range(COL_HALVES):
+                cols = slice(half * N_TILE, (half + 1) * N_TILE)
+                nc.tensor.matmul(
+                    out=spread[:, cols], lhsT=ones[:], rhs=bias_rows[gate][:, cols], start=True, stop=True
+                )
+            nc.scalar.copy(out=bias_all[gate][:], in_=spread[:])
+
+        for src, gates_after in (("x", ("i", "c")), ("h", ("f", "o"))):
             for m in range(ROW_TILES):
-                words = raw[src][:, m, :].bitcast(F32)
-                flipped = psum.tile([P, K_GROUPS * 2, P], F32, tag="bank")
-                for g in range(K_GROUPS):
-                    for u in range(2):
-                        first = g * (K_PASS // 2) + u
-                        nc.tensor.transpose(
-                            out=flipped[:, 2 * g + u, :],
-                            in_=words[:, first : (g + 1) * (K_PASS // 2) : 2],
-                            identity=identity[:],
-                        )
-                side_by_side = grouped[src][:, m, :].bitcast(F32).rearrange(
-                    "p (g b u) -> p g b u", g=K_GROUPS, u=2
+                transpose_and_regroup(src, m)
+                if m > 0:
+                    quantise(src, m - 1)
+            quantise(src, ROW_TILES - 1)
+            for gate in gates_after:
+                spread_bias(gate)
+
+        banks = [(half, gate, m) for half in range(COL_HALVES) for gate in GATES for m in range(ROW_TILES)]
+        passes = [(s, src, g) for s, src in enumerate(SOURCES) for g in range(K_GROUPS)]
+        value = {}
+
+        def multiply_and_activate(half, gate, m):
+            cols = slice(half * N_TILE, (half + 1) * N_TILE)
+            acc = psum.tile([P, N_TILE], F32, tag="bank")
+            for n, (s, src, g) in enumerate(passes):
+                k_cols = slice(g * P, (g + 1) * P)
+                plane_start = 4 * (K_GROUPS * s + g)
+                nc.tensor.matmul_mx(
+                    out=acc[:],
+                    lhsT=act_codes[src][:, m, k_cols].bitcast(FP8X4),
+                    lhsT_scale=act_scales[src][:, m, k_cols],
+                    rhs=w_words[(gate, src)][:, g, cols].bitcast(FP8X4),
+                    rhs_scale=w_planes[gate][plane_start:P, cols],
+                    start=(n == 0),
+                    stop=(n == len(passes) - 1),
                 )
-                permuted = flipped[:].rearrange("p (g u) b -> p g b u", u=2)
-                if m % 2 == 0:
-                    nc.vector.tensor_copy(out=side_by_side, in_=permuted)
-                else:
-                    nc.scalar.copy(out=side_by_side, in_=permuted)
-                nc.vector.quantize_mx(
-                    out=act_codes[src][:, m, :].bitcast(FP8X4),
-                    scales=act_scales[src][:, m, :],
-                    in_=grouped[src][:, m, :],
+            out_gate = work.tile([P, N_TILE], F32, name="gate_" + gate, tag="gate_" + gate)
+            value[(half, gate, m)] = out_gate
+            nc.vector.tensor_tensor(out=out_gate[:], in0=acc[:], in1=bias_all[gate][:, cols], op=ALU.add)
+            nc.scalar.activation(
+                out=out_gate[:], in_=out_gate[:], func=(ACT.Tanh if gate == "c" else ACT.Sigmoid)
+            )
+            if gate == "c":
+                nc.gpsimd.tensor_tensor(
+                    out=out_gate[:], in0=value[(half, "i", m)][:], in1=out_gate[:], op=ALU.mult
+                )
+            if gate == "f":
+                nc.gpsimd.tensor_tensor(
+                    out=out_gate[:], in0=out_gate[:], in1=c_sb[:, m, cols], op=ALU.mult
                 )
 
-        passes = [(s, src, g) for s, src in enumerate(SOURCES) for g in range(K_GROUPS)]
-        for half in range(COL_HALVES):
-            cols = slice(half * N_TILE, (half + 1) * N_TILE)
-            value = {}
-            for j, gate in enumerate(GATES):
-                for m in range(ROW_TILES):
-                    rows = slice(m * P, (m + 1) * P)
-                    acc = psum.tile([P, N_TILE], F32, tag="bank")
-                    for n, (s, src, g) in enumerate(passes):
-                        k_cols = slice(g * P, (g + 1) * P)
-                        plane_start = 4 * (K_GROUPS * s + g)
-                        nc.tensor.matmul_mx(
-                            out=acc[:],
-                            lhsT=act_codes[src][:, m, k_cols].bitcast(FP8X4),
-                            lhsT_scale=act_scales[src][:, m, k_cols],
-                            rhs=w_words[(gate, src)][:, g, cols].bitcast(FP8X4),
-                            rhs_scale=w_planes[gate][plane_start:P, cols],
-                            start=(n == 0),
-                            stop=(n == len(passes) - 1),
-                        )
-                    out_gate = work.tile([P, N_TILE], F32, name="gate_" + gate, tag="gate_" + gate)
-                    value[(gate, m)] = out_gate
-                    bias_cols = slice(j * HIDDEN + half * N_TILE, j * HIDDEN + (half + 1) * N_TILE)
-                    nc.vector.tensor_tensor(
-                        out=out_gate[:], in0=acc[:], in1=bias_all[:, bias_cols], op=ALU.add
-                    )
-                    nc.scalar.activation(
-                        out=out_gate[:], in_=out_gate[:], func=(ACT.Tanh if gate == "c" else ACT.Sigmoid)
-                    )
-                    if gate == "c":
-                        nc.gpsimd.tensor_tensor(
-                            out=out_gate[:], in0=value[("i", m)][:], in1=out_gate[:], op=ALU.mult
-                        )
-                    if gate == "f":
-                        nc.gpsimd.tensor_tensor(
-                            out=out_gate[:], in0=out_gate[:], in1=c_sb[:, m, cols], op=ALU.mult
-                        )
-                        nc.vector.tensor_tensor(
-                            out=out_gate[:], in0=out_gate[:], in1=value[("c", m)][:], op=ALU.add
-                        )
-                        nc.sync.dma_start(out=out_1[rows, cols], in_=out_gate[:])
-                        cell_tanh = work.tile([P, N_TILE], F32, tag="cell_tanh")
-                        value[("t", m)] = cell_tanh
-                        nc.scalar.activation(out=cell_tanh[:], in_=out_gate[:], func=ACT.Tanh)
-                    if gate == "o":
-                        nc.vector.tensor_tensor(
-                            out=out_gate[:], in0=out_gate[:], in1=value[("t", m)][:], op=ALU.mult
-                        )
-                        nc.sync.dma_start(out=out_0[rows, cols], in_=out_gate[:])
+        def finish_cell(half, m):
+            cell = value[(half, "f", m)]
+            nc.vector.tensor_tensor(out=cell[:], in0=cell[:], in1=value[(half, "c", m)][:], op=ALU.add)
+            nc.sync.dma_start(
+                out=out_1[m * P : (m + 1) * P, half * N_TILE : (half + 1) * N_TILE], in_=cell[:]
+            )
+            cell_tanh = work.tile([P, N_TILE], F32, tag="cell_tanh")
+            value[(half, "t", m)] = cell_tanh
+            nc.scalar.activation(out=cell_tanh[:], in_=cell[:], func=ACT.Tanh)
+
+        def finish_hidden(half, m):
+            hidden = value[(half, "o", m)]
+            nc.vector.tensor_tensor(out=hidden[:], in0=hidden[:], in1=value[(half, "t", m)][:], op=ALU.mult)
+            nc.sync.dma_start(
+                out=out_0[m * P : (m + 1) * P, half * N_TILE : (half + 1) * N_TILE], in_=hidden[:]
+            )
+
+        CELL_LAG = 2
+        HIDDEN_LAG = 1
+        for step in range(len(banks) + CELL_LAG):
+            if step < len(banks):
+                multiply_and_activate(*banks[step])
+            if step >= CELL_LAG and banks[step - CELL_LAG][1] == "f":
+                finish_cell(banks[step - CELL_LAG][0], banks[step - CELL_LAG][2])
+            if HIDDEN_LAG <= step < len(banks) + HIDDEN_LAG and banks[step - HIDDEN_LAG][1] == "o":
+                finish_hidden(banks[step - HIDDEN_LAG][0], banks[step - HIDDEN_LAG][2])

@@ -24,7 +24,7 @@ N_TILE = 512
 COL_HALVES = HIDDEN // N_TILE
 QUADRANTS = 4
 SOURCES = ("x", "h")
-GATES = ("i", "c", "f", "o")
+GATES = ("f", "i", "c", "o")
 
 FLOPS = 2 * BATCH * (2 * FEATURES) * (4 * HIDDEN)
 
@@ -95,23 +95,23 @@ def tile_lstmcell_kernel(
         table_warm = keep.tile([P, 1], F32)
 
         for gate in GATES:
-            nc.vector.memset(bias_rows[gate][:], 0.0)
-            nc.scalar.dma_start(out=bias_rows[gate][0:1, :], in_=dram_bias[gate].unsqueeze(0))
-        nc.vector.memset(ones[:], 1.0)
-        for gate in GATES:
             nc.vector.memset(w_planes[gate][:].bitcast(I32), 0)
+        for gate in GATES:
+            nc.vector.memset(bias_rows[gate][:], 0.0)
+        nc.vector.memset(ones[:], 1.0)
         nc.vector.memset(table_warm[:], 0.0)
         nc.scalar.activation(out=table_warm[:], in_=table_warm[:], func=ACT.Sigmoid)
         make_identity(nc, identity[:])
+        for gate in GATES:
+            nc.gpsimd.dma_start(out=bias_rows[gate][0:1, :], in_=dram_bias[gate].unsqueeze(0))
 
-        def load_scales(gate):
-            for s, src in enumerate(SOURCES):
-                for quad in range(QUADRANTS):
-                    first = 32 * quad + 4 * K_GROUPS * s
-                    nc.sync.dma_start(
-                        out=w_planes[gate][first : first + 4 * K_GROUPS, :].bitcast(I32),
-                        in_=dram_scales[(gate, src)][:, 4 * quad : 4 * quad + 4, :].bitcast(I32),
-                    )
+        def load_scales(gate, src):
+            for quad in range(QUADRANTS):
+                first = 32 * quad + 4 * K_GROUPS * SOURCES.index(src)
+                nc.sync.dma_start(
+                    out=w_planes[gate][first : first + 4 * K_GROUPS, :].bitcast(I32),
+                    in_=dram_scales[(gate, src)][:, 4 * quad : 4 * quad + 4, :].bitcast(I32),
+                )
 
         def load_words(gate, half):
             cols = slice(half * N_TILE, (half + 1) * N_TILE)
@@ -121,17 +121,28 @@ def tile_lstmcell_kernel(
                     out=w_words[(gate, src)][:, :, cols].bitcast(I32), in_=words[:, :, cols]
                 )
 
-        for src in SOURCES:
+        def load_activation(src):
             by_tile = activations[src].rearrange("(m p) k -> p m k", p=P)
             for first in range(0, ROW_TILES, 2):
                 nc.sync.dma_start(
                     out=raw[src][:, first : first + 2, :], in_=by_tile[:, first : first + 2, :]
                 )
-        for gate in GATES:
-            load_scales(gate)
-            load_words(gate, 0)
-            if gate == "f":
-                nc.sync.dma_start(out=c_sb[:], in_=c.rearrange("(m p) d -> p m d", p=P))
+
+        load_scales("f", "x")
+        load_activation("x")
+        load_scales("f", "h")
+        load_activation("h")
+        load_scales("i", "x")
+        load_words("f", 0)
+        load_scales("i", "h")
+        load_words("i", 0)
+        load_scales("c", "x")
+        nc.sync.dma_start(out=c_sb[:], in_=c.rearrange("(m p) d -> p m d", p=P))
+        load_scales("c", "h")
+        load_words("c", 0)
+        load_scales("o", "x")
+        load_words("o", 0)
+        load_scales("o", "h")
         for gate in GATES:
             load_words(gate, 1)
 
@@ -170,14 +181,12 @@ def tile_lstmcell_kernel(
                 )
             nc.scalar.copy(out=bias_all[gate][:], in_=spread[:])
 
-        for src, gates_after in (("x", ("i", "c")), ("h", ("f", "o"))):
+        for src in SOURCES:
             for m in range(ROW_TILES):
                 transpose_and_regroup(src, m)
                 if m > 0:
                     quantise(src, m - 1)
             quantise(src, ROW_TILES - 1)
-            for gate in gates_after:
-                spread_bias(gate)
 
         banks = [(half, gate, m) for half in range(COL_HALVES) for gate in GATES for m in range(ROW_TILES)]
         passes = [(s, src, g) for s, src in enumerate(SOURCES) for g in range(K_GROUPS)]
@@ -185,6 +194,8 @@ def tile_lstmcell_kernel(
 
         def multiply_and_activate(half, gate, m):
             cols = slice(half * N_TILE, (half + 1) * N_TILE)
+            if half == 0 and m == 0:
+                spread_bias(gate)
             acc = psum.tile([P, N_TILE], F32, tag="bank")
             for n, (s, src, g) in enumerate(passes):
                 k_cols = slice(g * P, (g + 1) * P)
@@ -214,8 +225,8 @@ def tile_lstmcell_kernel(
                 )
 
         def finish_cell(half, m):
-            cell = value[(half, "f", m)]
-            nc.vector.tensor_tensor(out=cell[:], in0=cell[:], in1=value[(half, "c", m)][:], op=ALU.add)
+            cell = value[(half, "c", m)]
+            nc.vector.tensor_tensor(out=cell[:], in0=cell[:], in1=value[(half, "f", m)][:], op=ALU.add)
             nc.sync.dma_start(
                 out=out_1[m * P : (m + 1) * P, half * N_TILE : (half + 1) * N_TILE], in_=cell[:]
             )
@@ -235,7 +246,7 @@ def tile_lstmcell_kernel(
         for step in range(len(banks) + CELL_LAG):
             if step < len(banks):
                 multiply_and_activate(*banks[step])
-            if step >= CELL_LAG and banks[step - CELL_LAG][1] == "f":
+            if step >= CELL_LAG and banks[step - CELL_LAG][1] == "c":
                 finish_cell(banks[step - CELL_LAG][0], banks[step - CELL_LAG][2])
             if HIDDEN_LAG <= step < len(banks) + HIDDEN_LAG and banks[step - HIDDEN_LAG][1] == "o":
                 finish_hidden(banks[step - HIDDEN_LAG][0], banks[step - HIDDEN_LAG][2])

@@ -121,17 +121,18 @@ def tile_lstmcell_kernel(
                     out=w_words[(gate, src)][:, :, cols].bitcast(I32), in_=words[:, :, cols]
                 )
 
-        def load_activation(src):
+        def load_activation(src, first, count):
             by_tile = activations[src].rearrange("(m p) k -> p m k", p=P)
-            for first in range(0, ROW_TILES, 2):
-                nc.sync.dma_start(
-                    out=raw[src][:, first : first + 2, :], in_=by_tile[:, first : first + 2, :]
-                )
+            tiles = slice(first, first + count)
+            nc.sync.dma_start(out=raw[src][:, tiles, :], in_=by_tile[:, tiles, :])
 
+        load_activation("x", 0, 1)
+        load_activation("x", 1, 1)
         load_scales("f", "x")
-        load_activation("x")
+        load_activation("x", 2, 2)
+        load_activation("h", 0, 2)
         load_scales("f", "h")
-        load_activation("h")
+        load_activation("h", 2, 2)
         load_scales("i", "x")
         load_words("f", 0)
         load_scales("i", "h")
@@ -234,19 +235,26 @@ def tile_lstmcell_kernel(
             value[(half, "t", m)] = cell_tanh
             nc.scalar.activation(out=cell_tanh[:], in_=cell[:], func=ACT.Tanh)
 
-        def finish_hidden(half, m):
+        def finish_hidden(half, m, engine):
             hidden = value[(half, "o", m)]
-            nc.vector.tensor_tensor(out=hidden[:], in0=hidden[:], in1=value[(half, "t", m)][:], op=ALU.mult)
+            engine.tensor_tensor(out=hidden[:], in0=hidden[:], in1=value[(half, "t", m)][:], op=ALU.mult)
             nc.sync.dma_start(
                 out=out_0[m * P : (m + 1) * P, half * N_TILE : (half + 1) * N_TILE], in_=hidden[:]
             )
 
-        CELL_LAG = 2
-        HIDDEN_LAG = 1
+        CELL_LAG = 3
+        HIDDEN_LAG = 2
         for step in range(len(banks) + CELL_LAG):
             if step < len(banks):
-                multiply_and_activate(*banks[step])
-            if step >= CELL_LAG and banks[step - CELL_LAG][1] == "c":
-                finish_cell(banks[step - CELL_LAG][0], banks[step - CELL_LAG][2])
-            if HIDDEN_LAG <= step < len(banks) + HIDDEN_LAG and banks[step - HIDDEN_LAG][1] == "o":
-                finish_hidden(banks[step - HIDDEN_LAG][0], banks[step - HIDDEN_LAG][2])
+                half, gate, m = banks[step]
+                multiply_and_activate(half, gate, m)
+                if gate == "o" and m % 2 == 0:
+                    finish_hidden(half, m, nc.gpsimd)
+            if step >= CELL_LAG:
+                half, gate, m = banks[step - CELL_LAG]
+                if gate == "c":
+                    finish_cell(half, m)
+            if HIDDEN_LAG <= step < len(banks) + HIDDEN_LAG:
+                half, gate, m = banks[step - HIDDEN_LAG]
+                if gate == "o" and m % 2 == 1:
+                    finish_hidden(half, m, nc.vector)

@@ -28,6 +28,19 @@ GATES = ("f", "i", "c", "o")
 
 FLOPS = 2 * BATCH * (2 * FEATURES) * (4 * HIDDEN)
 
+BIAS_HEAD = False
+FIRST_SRC_MAJOR = True
+LAST_PIECES = (512,)
+LOAD_ORDER = "A"
+ENG_FC = "g"
+ENG_IC = "g"
+ENG_HO_EVEN = "g"
+COPY_ENGINES = ("v", "s")
+CELL_LAG = 3
+HIDDEN_LAG = 2
+PROD_LAG = 1
+WORK_BUFS = 6
+
 
 def tile_lstmcell_kernel(
     tc,
@@ -54,10 +67,11 @@ def tile_lstmcell_kernel(
         ("c", "x"): W_xc_scales, ("c", "h"): W_hc_scales,
     }
     dram_bias = {"i": b_i, "f": b_f, "o": b_o, "c": b_c}
+    engines = {"g": nc.gpsimd, "v": nc.vector, "s": nc.scalar}
 
     with ExitStack() as stack:
         keep = stack.enter_context(tc.tile_pool(name="keep", bufs=1))
-        work = stack.enter_context(tc.tile_pool(name="work", bufs=6))
+        work = stack.enter_context(tc.tile_pool(name="work", bufs=WORK_BUFS))
         psum = stack.enter_context(tc.psum_pool(name="psum", bufs=8))
         stack.enter_context(tc.manual_schedule())
 
@@ -113,39 +127,69 @@ def tile_lstmcell_kernel(
                     in_=dram_scales[(gate, src)][:, 4 * quad : 4 * quad + 4, :].bitcast(I32),
                 )
 
-        def load_words(gate, half):
+        def load_words_of(gate, src, half):
             cols = slice(half * N_TILE, (half + 1) * N_TILE)
+            words = dram_words[(gate, src)].rearrange("g p n t -> p g (n t)").bitcast(I32)
+            nc.sync.dma_start(
+                out=w_words[(gate, src)][:, :, cols].bitcast(I32), in_=words[:, :, cols]
+            )
+
+        def load_words(gate, half):
             for src in SOURCES:
-                words = dram_words[(gate, src)].rearrange("g p n t -> p g (n t)").bitcast(I32)
-                nc.sync.dma_start(
-                    out=w_words[(gate, src)][:, :, cols].bitcast(I32), in_=words[:, :, cols]
-                )
+                load_words_of(gate, src, half)
 
         def load_activation(src, first, count):
             by_tile = activations[src].rearrange("(m p) k -> p m k", p=P)
             tiles = slice(first, first + count)
             nc.sync.dma_start(out=raw[src][:, tiles, :], in_=by_tile[:, tiles, :])
 
-        load_activation("x", 0, 1)
-        load_activation("x", 1, 1)
-        load_scales("f", "x")
-        load_activation("x", 2, 2)
-        load_activation("h", 0, 2)
-        load_scales("f", "h")
-        load_activation("h", 2, 2)
-        load_scales("i", "x")
-        load_words("f", 0)
-        load_scales("i", "h")
-        load_words("i", 0)
-        load_scales("c", "x")
-        nc.sync.dma_start(out=c_sb[:], in_=c.rearrange("(m p) d -> p m d", p=P))
-        load_scales("c", "h")
-        load_words("c", 0)
-        load_scales("o", "x")
-        load_words("o", 0)
-        load_scales("o", "h")
-        for gate in GATES:
-            load_words(gate, 1)
+        def load_cell():
+            nc.sync.dma_start(out=c_sb[:], in_=c.rearrange("(m p) d -> p m d", p=P))
+
+        if LOAD_ORDER == "base":
+            load_activation("x", 0, 1)
+            load_activation("x", 1, 1)
+            load_scales("f", "x")
+            load_activation("x", 2, 2)
+            load_activation("h", 0, 2)
+            load_scales("f", "h")
+            load_activation("h", 2, 2)
+            load_scales("i", "x")
+            load_words("f", 0)
+            load_scales("i", "h")
+            load_words("i", 0)
+            load_scales("c", "x")
+            load_cell()
+            load_scales("c", "h")
+            load_words("c", 0)
+            load_scales("o", "x")
+            load_words("o", 0)
+            load_scales("o", "h")
+            for gate in GATES:
+                load_words(gate, 1)
+        if LOAD_ORDER == "A":
+            load_activation("x", 0, 1)
+            load_activation("x", 1, 1)
+            load_scales("f", "x")
+            load_activation("x", 2, 2)
+            load_activation("h", 0, 2)
+            load_activation("h", 2, 2)
+            load_words_of("f", "x", 0)
+            load_scales("f", "h")
+            load_words_of("f", "h", 0)
+            load_scales("i", "x")
+            load_words_of("i", "x", 0)
+            load_scales("i", "h")
+            load_words_of("i", "h", 0)
+            load_scales("c", "x")
+            load_cell()
+            load_scales("c", "h")
+            load_words("c", 0)
+            load_scales("o", "x")
+            load_words("o", 0)
+            load_scales("o", "h")
+            for gate in GATES:
+                load_words(gate, 1)
 
         def transpose_and_regroup(src, m):
             words = raw[src][:, m, :].bitcast(F32)
@@ -161,7 +205,7 @@ def tile_lstmcell_kernel(
                 "p (g b u) -> p g b u", g=K_GROUPS, u=2
             )
             permuted = flipped[:].rearrange("p (g u) b -> p g b u", u=2)
-            if m % 2 == 0:
+            if COPY_ENGINES[m % 2] == "v":
                 nc.vector.tensor_copy(out=side_by_side, in_=permuted)
             else:
                 nc.scalar.copy(out=side_by_side, in_=permuted)
@@ -188,42 +232,78 @@ def tile_lstmcell_kernel(
                 if m > 0:
                     quantise(src, m - 1)
             quantise(src, ROW_TILES - 1)
+            if BIAS_HEAD and src == "x":
+                spread_bias("f")
+        if BIAS_HEAD:
+            for gate in GATES[1:]:
+                spread_bias(gate)
 
         banks = [(half, gate, m) for half in range(COL_HALVES) for gate in GATES for m in range(ROW_TILES)]
         passes = [(s, src, g) for s, src in enumerate(SOURCES) for g in range(K_GROUPS)]
         value = {}
+        open_acc = {}
 
-        def multiply_and_activate(half, gate, m):
-            cols = slice(half * N_TILE, (half + 1) * N_TILE)
-            if half == 0 and m == 0:
-                spread_bias(gate)
-            acc = psum.tile([P, N_TILE], F32, tag="bank")
-            for n, (s, src, g) in enumerate(passes):
+        def multiply(acc, half, gate, m, first_col, width, chosen):
+            cols = slice(half * N_TILE + first_col, half * N_TILE + first_col + width)
+            for s, src, g in chosen:
+                n = K_GROUPS * s + g
                 k_cols = slice(g * P, (g + 1) * P)
-                plane_start = 4 * (K_GROUPS * s + g)
                 nc.tensor.matmul_mx(
                     out=acc[:],
                     lhsT=act_codes[src][:, m, k_cols].bitcast(FP8X4),
                     lhsT_scale=act_scales[src][:, m, k_cols],
                     rhs=w_words[(gate, src)][:, g, cols].bitcast(FP8X4),
-                    rhs_scale=w_planes[gate][plane_start:P, cols],
+                    rhs_scale=w_planes[gate][4 * n : P, cols],
                     start=(n == 0),
                     stop=(n == len(passes) - 1),
                 )
-            out_gate = work.tile([P, N_TILE], F32, name="gate_" + gate, tag="gate_" + gate)
-            value[(half, gate, m)] = out_gate
-            nc.vector.tensor_tensor(out=out_gate[:], in0=acc[:], in1=bias_all[gate][:, cols], op=ALU.add)
-            nc.scalar.activation(
-                out=out_gate[:], in_=out_gate[:], func=(ACT.Tanh if gate == "c" else ACT.Sigmoid)
-            )
+
+        def add_bias(acc, half, gate, m, first_col, width):
+            cols = slice(half * N_TILE + first_col, half * N_TILE + first_col + width)
+            part = value[(half, gate, m)][:, first_col : first_col + width]
+            nc.vector.tensor_tensor(out=part, in0=acc[:], in1=bias_all[gate][:, cols], op=ALU.add)
+
+        def activate(half, gate, m, first_col, width):
+            part = value[(half, gate, m)][:, first_col : first_col + width]
+            nc.scalar.activation(out=part, in_=part, func=(ACT.Tanh if gate == "c" else ACT.Sigmoid))
+
+        def product(half, gate, m, engine):
+            out_gate = value[(half, gate, m)]
+            cols = slice(half * N_TILE, (half + 1) * N_TILE)
             if gate == "c":
-                nc.gpsimd.tensor_tensor(
+                engine.tensor_tensor(
                     out=out_gate[:], in0=value[(half, "i", m)][:], in1=out_gate[:], op=ALU.mult
                 )
             if gate == "f":
-                nc.gpsimd.tensor_tensor(
+                engine.tensor_tensor(
                     out=out_gate[:], in0=out_gate[:], in1=c_sb[:, m, cols], op=ALU.mult
                 )
+
+        def new_gate_tile(half, gate, m):
+            out_gate = work.tile([P, N_TILE], F32, name="gate_" + gate, tag="gate_" + gate)
+            value[(half, gate, m)] = out_gate
+
+        def multiply_and_activate(step):
+            half, gate, m = banks[step]
+            if half == 0 and m == 0 and not BIAS_HEAD:
+                spread_bias(gate)
+            new_gate_tile(half, gate, m)
+            if FIRST_SRC_MAJOR and step < ROW_TILES:
+                if step == 0:
+                    for mm in range(ROW_TILES):
+                        open_acc[mm] = psum.tile([P, N_TILE], F32, name="acc_first", tag="bank")
+                        multiply(open_acc[mm], half, gate, mm, 0, N_TILE, passes[:K_GROUPS])
+                acc = open_acc[m]
+                multiply(acc, half, gate, m, 0, N_TILE, passes[K_GROUPS:])
+            else:
+                acc = psum.tile([P, N_TILE], F32, tag="bank")
+                multiply(acc, half, gate, m, 0, N_TILE, passes)
+            add_bias(acc, half, gate, m, 0, N_TILE)
+            activate(half, gate, m, 0, N_TILE)
+            if gate == "c" and ENG_IC == "g":
+                product(half, gate, m, nc.gpsimd)
+            if gate == "f" and ENG_FC == "g":
+                product(half, gate, m, nc.gpsimd)
 
         def finish_cell(half, m):
             cell = value[(half, "c", m)]
@@ -235,26 +315,49 @@ def tile_lstmcell_kernel(
             value[(half, "t", m)] = cell_tanh
             nc.scalar.activation(out=cell_tanh[:], in_=cell[:], func=ACT.Tanh)
 
-        def finish_hidden(half, m, engine):
+        def finish_hidden(half, m, engine, first_col, width):
+            part = slice(first_col, first_col + width)
             hidden = value[(half, "o", m)]
-            engine.tensor_tensor(out=hidden[:], in0=hidden[:], in1=value[(half, "t", m)][:], op=ALU.mult)
+            engine.tensor_tensor(
+                out=hidden[:, part], in0=hidden[:, part], in1=value[(half, "t", m)][:, part], op=ALU.mult
+            )
             nc.sync.dma_start(
-                out=out_0[m * P : (m + 1) * P, half * N_TILE : (half + 1) * N_TILE], in_=hidden[:]
+                out=out_0[m * P : (m + 1) * P, half * N_TILE + first_col : half * N_TILE + first_col + width],
+                in_=hidden[:, part],
             )
 
-        CELL_LAG = 3
-        HIDDEN_LAG = 2
+        last = len(banks) - 1
         for step in range(len(banks) + CELL_LAG):
-            if step < len(banks):
+            if step < last:
                 half, gate, m = banks[step]
-                multiply_and_activate(half, gate, m)
-                if gate == "o" and m % 2 == 0:
-                    finish_hidden(half, m, nc.gpsimd)
+                multiply_and_activate(step)
+                if gate == "o" and m % 2 == 0 and ENG_HO_EVEN == "g":
+                    finish_hidden(half, m, nc.gpsimd, 0, N_TILE)
+            if PROD_LAG <= step < len(banks) + PROD_LAG:
+                half, gate, m = banks[step - PROD_LAG]
+                if gate == "c" and ENG_IC == "v":
+                    product(half, gate, m, nc.vector)
+                if gate == "f" and ENG_FC == "v":
+                    product(half, gate, m, nc.vector)
             if step >= CELL_LAG:
                 half, gate, m = banks[step - CELL_LAG]
                 if gate == "c":
                     finish_cell(half, m)
-            if HIDDEN_LAG <= step < len(banks) + HIDDEN_LAG:
+            if HIDDEN_LAG <= step < last + HIDDEN_LAG:
                 half, gate, m = banks[step - HIDDEN_LAG]
-                if gate == "o" and m % 2 == 1:
-                    finish_hidden(half, m, nc.vector)
+                if gate == "o" and (m % 2 == 1 or ENG_HO_EVEN == "v"):
+                    finish_hidden(half, m, nc.vector, 0, N_TILE)
+            if step == last:
+                half, gate, m = banks[step]
+                new_gate_tile(half, gate, m)
+                starts = [sum(LAST_PIECES[:j]) for j in range(len(LAST_PIECES))]
+                for first_col, width in zip(starts, LAST_PIECES):
+                    piece = psum.tile([P, width], F32, name="piece", tag="bank")
+                    multiply(piece, half, gate, m, first_col, width, passes)
+                    add_bias(piece, half, gate, m, first_col, width)
+                    activate(half, gate, m, first_col, width)
+            if step == last + 1:
+                half, gate, m = banks[last]
+                starts = [sum(LAST_PIECES[:j]) for j in range(len(LAST_PIECES))]
+                for first_col, width in zip(starts, LAST_PIECES):
+                    finish_hidden(half, m, nc.vector, first_col, width)

@@ -40,6 +40,9 @@ CELL_LAG = 3
 HIDDEN_LAG = 2
 PROD_LAG = 1
 WORK_BUFS = 6
+BIAS_MODE = "pe"
+WARM_START = 4
+WARM_BETWEEN = 1
 
 
 def tile_lstmcell_kernel(
@@ -104,20 +107,35 @@ def tile_lstmcell_kernel(
             bias_rows[gate] = keep.tile([P, HIDDEN], BF16, name="bias_rows_" + gate)
             bias_all[gate] = keep.tile([P, HIDDEN], BF16, name="bias_all_" + gate)
         c_sb = keep.tile([P, ROW_TILES, HIDDEN], BF16)
-        ones = keep.tile([P, P], BF16)
+        ones = keep.tile([P, N_TILE], BF16)
         identity = keep.tile([P, P], F32)
         table_warm = keep.tile([P, 1], F32)
 
+        if WARM_START or WARM_BETWEEN:
+            nc.vector.memset(ones[:], 1.0)
         for gate in GATES:
             nc.vector.memset(w_planes[gate][:].bitcast(I32), 0)
-        for gate in GATES:
-            nc.vector.memset(bias_rows[gate][:], 0.0)
-        nc.vector.memset(ones[:], 1.0)
+        if BIAS_MODE == "pe":
+            for gate in GATES:
+                nc.vector.memset(bias_rows[gate][:], 0.0)
+            if not (WARM_START or WARM_BETWEEN):
+                nc.vector.memset(ones[:], 1.0)
         nc.vector.memset(table_warm[:], 0.0)
         nc.scalar.activation(out=table_warm[:], in_=table_warm[:], func=ACT.Sigmoid)
         make_identity(nc, identity[:])
         for gate in GATES:
-            nc.gpsimd.dma_start(out=bias_rows[gate][0:1, :], in_=dram_bias[gate].unsqueeze(0))
+            if BIAS_MODE == "pe":
+                nc.gpsimd.dma_start(out=bias_rows[gate][0:1, :], in_=dram_bias[gate].unsqueeze(0))
+            if BIAS_MODE == "dma_g":
+                nc.gpsimd.dma_start(out=bias_all[gate][:], in_=dram_bias[gate].partition_broadcast(P))
+
+        def warm(count):
+            if count > 0:
+                unread = psum.tile([P, N_TILE], F32, name="unread", tag="bank")
+                for j in range(count):
+                    nc.tensor.matmul(out=unread[:], lhsT=ones[:, 0:P], rhs=ones[:], start=True, stop=True)
+
+        warm(WARM_START)
 
         def load_scales(gate, src):
             for quad in range(QUADRANTS):
@@ -142,6 +160,10 @@ def tile_lstmcell_kernel(
             by_tile = activations[src].rearrange("(m p) k -> p m k", p=P)
             tiles = slice(first, first + count)
             nc.sync.dma_start(out=raw[src][:, tiles, :], in_=by_tile[:, tiles, :])
+
+        def load_bias(gate):
+            if BIAS_MODE == "dma_s":
+                nc.sync.dma_start(out=bias_all[gate][:], in_=dram_bias[gate].partition_broadcast(P))
 
         def load_cell():
             nc.sync.dma_start(out=c_sb[:], in_=c.rearrange("(m p) d -> p m d", p=P))
@@ -222,19 +244,20 @@ def tile_lstmcell_kernel(
             for half in range(COL_HALVES):
                 cols = slice(half * N_TILE, (half + 1) * N_TILE)
                 nc.tensor.matmul(
-                    out=spread[:, cols], lhsT=ones[:], rhs=bias_rows[gate][:, cols], start=True, stop=True
+                    out=spread[:, cols], lhsT=ones[:, 0:P], rhs=bias_rows[gate][:, cols], start=True, stop=True
                 )
             nc.scalar.copy(out=bias_all[gate][:], in_=spread[:])
 
         for src in SOURCES:
             for m in range(ROW_TILES):
                 transpose_and_regroup(src, m)
+                warm(WARM_BETWEEN)
                 if m > 0:
                     quantise(src, m - 1)
             quantise(src, ROW_TILES - 1)
-            if BIAS_HEAD and src == "x":
+            if BIAS_HEAD and src == "x" and BIAS_MODE == "pe":
                 spread_bias("f")
-        if BIAS_HEAD:
+        if BIAS_HEAD and BIAS_MODE == "pe":
             for gate in GATES[1:]:
                 spread_bias(gate)
 
@@ -285,7 +308,7 @@ def tile_lstmcell_kernel(
 
         def multiply_and_activate(step):
             half, gate, m = banks[step]
-            if half == 0 and m == 0 and not BIAS_HEAD:
+            if half == 0 and m == 0 and not BIAS_HEAD and BIAS_MODE == "pe":
                 spread_bias(gate)
             new_gate_tile(half, gate, m)
             if FIRST_SRC_MAJOR and step < ROW_TILES:

@@ -22,27 +22,14 @@ K_GROUPS = FEATURES // K_PASS
 ROW_TILES = BATCH // P
 N_TILE = 512
 COL_HALVES = HIDDEN // N_TILE
+D_TILES = N_TILE // P
 QUADRANTS = 4
 SOURCES = ("x", "h")
 GATES = ("f", "i", "c", "o")
+ROW_GATES = ("f", "o")
+COL_GATES = ("i", "c")
 
 FLOPS = 2 * BATCH * (2 * FEATURES) * (4 * HIDDEN)
-
-BIAS_HEAD = False
-FIRST_SRC_MAJOR = True
-LAST_PIECES = (512,)
-LOAD_ORDER = "A"
-ENG_FC = "g"
-ENG_IC = "g"
-ENG_HO_EVEN = "g"
-COPY_ENGINES = ("v", "s")
-CELL_LAG = 3
-HIDDEN_LAG = 2
-PROD_LAG = 1
-WORK_BUFS = 6
-BIAS_MODE = "pe"
-WARM_START = 4
-WARM_BETWEEN = 1
 
 
 def tile_lstmcell_kernel(
@@ -70,11 +57,10 @@ def tile_lstmcell_kernel(
         ("c", "x"): W_xc_scales, ("c", "h"): W_hc_scales,
     }
     dram_bias = {"i": b_i, "f": b_f, "o": b_o, "c": b_c}
-    engines = {"g": nc.gpsimd, "v": nc.vector, "s": nc.scalar}
 
     with ExitStack() as stack:
         keep = stack.enter_context(tc.tile_pool(name="keep", bufs=1))
-        work = stack.enter_context(tc.tile_pool(name="work", bufs=WORK_BUFS))
+        work = stack.enter_context(tc.tile_pool(name="work", bufs=6))
         psum = stack.enter_context(tc.psum_pool(name="psum", bufs=8))
         stack.enter_context(tc.manual_schedule())
 
@@ -85,14 +71,10 @@ def tile_lstmcell_kernel(
         for src in SOURCES:
             raw[src] = keep.tile([P, ROW_TILES, FEATURES], BF16, name="raw_" + src)
             grouped[src] = keep.tile(
-                [P, ROW_TILES, K_GROUPS * P * PACK], BF16, name="grouped_" + src, align_bytes=64
+                [P, K_GROUPS, BATCH * PACK], BF16, name="grouped_" + src, align_bytes=64
             )
-            act_codes[src] = keep.tile(
-                [P, ROW_TILES, K_GROUPS * P], U32, name="codes_" + src, align_bytes=64
-            )
-            act_scales[src] = keep.tile(
-                [P, ROW_TILES, K_GROUPS * P], U8, name="scales_" + src, align_bytes=64
-            )
+            act_codes[src] = keep.tile([P, K_GROUPS, BATCH], U32, name="codes_" + src, align_bytes=64)
+            act_scales[src] = keep.tile([P, K_GROUPS, BATCH], U8, name="scales_" + src, align_bytes=64)
         w_words = {}
         for gate in GATES:
             for src in SOURCES:
@@ -100,42 +82,44 @@ def tile_lstmcell_kernel(
                     [P, K_GROUPS, HIDDEN], U32, name="w_" + src + gate, align_bytes=64
                 )
         w_planes = {}
-        bias_rows = {}
-        bias_all = {}
         for gate in GATES:
             w_planes[gate] = keep.tile([P, HIDDEN], U8, name="planes_" + gate, align_bytes=64)
+        bias_rows = {}
+        bias_all = {}
+        for gate in ROW_GATES:
             bias_rows[gate] = keep.tile([P, HIDDEN], BF16, name="bias_rows_" + gate)
             bias_all[gate] = keep.tile([P, HIDDEN], BF16, name="bias_all_" + gate)
+        bias_square = keep.tile([P, P], BF16, name="bias_square")
+        bias_cols = keep.tile([P, P], F32, name="bias_cols")
         c_sb = keep.tile([P, ROW_TILES, HIDDEN], BF16)
-        ones = keep.tile([P, N_TILE], BF16)
+        ones = keep.tile([P, P], BF16)
         identity = keep.tile([P, P], F32)
+        identity_bf = keep.tile([P, P], BF16)
         table_warm = keep.tile([P, 1], F32)
 
-        if WARM_START or WARM_BETWEEN:
-            nc.vector.memset(ones[:], 1.0)
         for gate in GATES:
             nc.vector.memset(w_planes[gate][:].bitcast(I32), 0)
-        if BIAS_MODE == "pe":
-            for gate in GATES:
-                nc.vector.memset(bias_rows[gate][:], 0.0)
-            if not (WARM_START or WARM_BETWEEN):
-                nc.vector.memset(ones[:], 1.0)
+        nc.vector.memset(bias_square[:].bitcast(I32), 0)
+        for gate in ROW_GATES:
+            nc.vector.memset(bias_rows[gate][:].bitcast(I32), 0)
+        nc.vector.memset(ones[:], 1.0)
         nc.vector.memset(table_warm[:], 0.0)
         nc.scalar.activation(out=table_warm[:], in_=table_warm[:], func=ACT.Sigmoid)
         make_identity(nc, identity[:])
-        for gate in GATES:
-            if BIAS_MODE == "pe":
+        nc.vector.tensor_copy(out=identity_bf[:], in_=identity[:])
+
+        def load_bias(gate):
+            if gate in ROW_GATES:
                 nc.gpsimd.dma_start(out=bias_rows[gate][0:1, :], in_=dram_bias[gate].unsqueeze(0))
-            if BIAS_MODE == "dma_g":
-                nc.gpsimd.dma_start(out=bias_all[gate][:], in_=dram_bias[gate].partition_broadcast(P))
+            else:
+                first = (HIDDEN // P) * COL_GATES.index(gate)
+                nc.gpsimd.dma_start(
+                    out=bias_square[first : first + HIDDEN // P, :],
+                    in_=dram_bias[gate].rearrange("(j p) -> j p", p=P),
+                )
 
-        def warm(count):
-            if count > 0:
-                unread = psum.tile([P, N_TILE], F32, name="unread", tag="bank")
-                for j in range(count):
-                    nc.tensor.matmul(out=unread[:], lhsT=ones[:, 0:P], rhs=ones[:], start=True, stop=True)
-
-        warm(WARM_START)
+        for gate in GATES:
+            load_bias(gate)
 
         def load_scales(gate, src):
             for quad in range(QUADRANTS):
@@ -145,77 +129,47 @@ def tile_lstmcell_kernel(
                     in_=dram_scales[(gate, src)][:, 4 * quad : 4 * quad + 4, :].bitcast(I32),
                 )
 
-        def load_words_of(gate, src, half):
+        def load_words(gate, src, half):
             cols = slice(half * N_TILE, (half + 1) * N_TILE)
             words = dram_words[(gate, src)].rearrange("g p n t -> p g (n t)").bitcast(I32)
             nc.sync.dma_start(
                 out=w_words[(gate, src)][:, :, cols].bitcast(I32), in_=words[:, :, cols]
             )
 
-        def load_words(gate, half):
-            for src in SOURCES:
-                load_words_of(gate, src, half)
-
         def load_activation(src, first, count):
             by_tile = activations[src].rearrange("(m p) k -> p m k", p=P)
             tiles = slice(first, first + count)
             nc.sync.dma_start(out=raw[src][:, tiles, :], in_=by_tile[:, tiles, :])
 
-        def load_bias(gate):
-            if BIAS_MODE == "dma_s":
-                nc.sync.dma_start(out=bias_all[gate][:], in_=dram_bias[gate].partition_broadcast(P))
-
-        def load_cell():
-            nc.sync.dma_start(out=c_sb[:], in_=c.rearrange("(m p) d -> p m d", p=P))
-
-        if LOAD_ORDER == "base":
-            load_activation("x", 0, 1)
-            load_activation("x", 1, 1)
-            load_scales("f", "x")
-            load_activation("x", 2, 2)
-            load_activation("h", 0, 2)
-            load_scales("f", "h")
-            load_activation("h", 2, 2)
-            load_scales("i", "x")
-            load_words("f", 0)
-            load_scales("i", "h")
-            load_words("i", 0)
-            load_scales("c", "x")
-            load_cell()
-            load_scales("c", "h")
-            load_words("c", 0)
-            load_scales("o", "x")
-            load_words("o", 0)
-            load_scales("o", "h")
-            for gate in GATES:
-                load_words(gate, 1)
-        if LOAD_ORDER == "A":
-            load_activation("x", 0, 1)
-            load_activation("x", 1, 1)
-            load_scales("f", "x")
-            load_activation("x", 2, 2)
-            load_activation("h", 0, 2)
-            load_activation("h", 2, 2)
-            load_words_of("f", "x", 0)
-            load_scales("f", "h")
-            load_words_of("f", "h", 0)
-            load_scales("i", "x")
-            load_words_of("i", "x", 0)
-            load_scales("i", "h")
-            load_words_of("i", "h", 0)
-            load_scales("c", "x")
-            load_cell()
-            load_scales("c", "h")
-            load_words("c", 0)
-            load_scales("o", "x")
-            load_words("o", 0)
-            load_scales("o", "h")
-            for gate in GATES:
-                load_words(gate, 1)
+        load_activation("x", 0, 1)
+        load_activation("x", 1, 1)
+        load_scales("f", "x")
+        load_activation("x", 2, 2)
+        load_activation("h", 0, 2)
+        load_activation("h", 2, 2)
+        load_words("f", "x", 0)
+        load_scales("f", "h")
+        load_words("f", "h", 0)
+        load_scales("i", "x")
+        load_words("i", "x", 0)
+        load_scales("i", "h")
+        load_words("i", "h", 0)
+        load_scales("c", "x")
+        nc.sync.dma_start(out=c_sb[:], in_=c.rearrange("(m p) d -> p m d", p=P))
+        load_scales("c", "h")
+        load_words("c", "x", 0)
+        load_words("c", "h", 0)
+        load_scales("o", "x")
+        load_words("o", "x", 0)
+        load_words("o", "h", 0)
+        load_scales("o", "h")
+        for gate in GATES:
+            for src in SOURCES:
+                load_words(gate, src, 1)
 
         def transpose_and_regroup(src, m):
             words = raw[src][:, m, :].bitcast(F32)
-            flipped = psum.tile([P, K_GROUPS * 2, P], F32, tag="bank")
+            flipped = psum.tile([P, K_GROUPS * 2, P], F32, name="flipped", tag="bank")
             for g in range(K_GROUPS):
                 for u in range(2):
                     nc.tensor.transpose(
@@ -223,164 +177,194 @@ def tile_lstmcell_kernel(
                         in_=words[:, g * (K_PASS // 2) + u : (g + 1) * (K_PASS // 2) : 2],
                         identity=identity[:],
                     )
-            side_by_side = grouped[src][:, m, :].bitcast(F32).rearrange(
-                "p (g b u) -> p g b u", g=K_GROUPS, u=2
-            )
+            side_by_side = grouped[src][:].bitcast(F32).rearrange("p g (b u) -> p g b u", u=2)
+            side_by_side = side_by_side[:, :, m * P : (m + 1) * P, :]
             permuted = flipped[:].rearrange("p (g u) b -> p g b u", u=2)
-            if COPY_ENGINES[m % 2] == "v":
+            if m % 2 == 0:
                 nc.vector.tensor_copy(out=side_by_side, in_=permuted)
             else:
                 nc.scalar.copy(out=side_by_side, in_=permuted)
 
-        def quantise(src, m):
-            nc.vector.quantize_mx(
-                out=act_codes[src][:, m, :].bitcast(FP8X4),
-                scales=act_scales[src][:, m, :],
-                in_=grouped[src][:, m, :],
-            )
+        def quantise(src, first_tile, tiles):
+            rows = slice(first_tile * P, (first_tile + tiles) * P)
+            for g in range(K_GROUPS):
+                nc.vector.quantize_mx(
+                    out=act_codes[src][:, g, rows].bitcast(FP8X4),
+                    scales=act_scales[src][:, g, rows],
+                    in_=grouped[src][:, g, first_tile * P * PACK : (first_tile + tiles) * P * PACK],
+                )
 
         def spread_bias(gate):
-            spread = psum.tile([P, HIDDEN], BF16, tag="bank")
+            spread = psum.tile([P, HIDDEN], BF16, name="spread", tag="bank")
             for half in range(COL_HALVES):
                 cols = slice(half * N_TILE, (half + 1) * N_TILE)
                 nc.tensor.matmul(
-                    out=spread[:, cols], lhsT=ones[:, 0:P], rhs=bias_rows[gate][:, cols], start=True, stop=True
+                    out=spread[:, cols], lhsT=ones[:], rhs=bias_rows[gate][:, cols], start=True, stop=True
                 )
             nc.scalar.copy(out=bias_all[gate][:], in_=spread[:])
+
+        def turn_bias_square():
+            turned = psum.tile([P, P], BF16, name="turned", tag="bank")
+            nc.tensor.transpose(out=turned[:], in_=bias_square[:], identity=identity_bf[:])
+            nc.scalar.copy(out=bias_cols[:], in_=turned[:])
 
         for src in SOURCES:
             for m in range(ROW_TILES):
                 transpose_and_regroup(src, m)
-                warm(WARM_BETWEEN)
-                if m > 0:
-                    quantise(src, m - 1)
-            quantise(src, ROW_TILES - 1)
-            if BIAS_HEAD and src == "x" and BIAS_MODE == "pe":
-                spread_bias("f")
-        if BIAS_HEAD and BIAS_MODE == "pe":
-            for gate in GATES[1:]:
-                spread_bias(gate)
+                if m == 2:
+                    quantise(src, 0, 2)
+                if m == 0 and src == "h":
+                    quantise("x", 2, 2)
+        quantise("h", 2, 2)
 
-        banks = [(half, gate, m) for half in range(COL_HALVES) for gate in GATES for m in range(ROW_TILES)]
-        passes = [(s, src, g) for s, src in enumerate(SOURCES) for g in range(K_GROUPS)]
+        passes = [(SOURCES.index(src), src, g) for src in SOURCES for g in range(K_GROUPS)]
         value = {}
-        open_acc = {}
+        product_bank = {}
 
-        def multiply(acc, half, gate, m, first_col, width, chosen):
-            cols = slice(half * N_TILE + first_col, half * N_TILE + first_col + width)
+        def row_passes(acc, gate, half, m, chosen):
+            rows = slice(m * P, (m + 1) * P)
+            cols = slice(half * N_TILE, (half + 1) * N_TILE)
             for s, src, g in chosen:
                 n = K_GROUPS * s + g
-                k_cols = slice(g * P, (g + 1) * P)
                 nc.tensor.matmul_mx(
                     out=acc[:],
-                    lhsT=act_codes[src][:, m, k_cols].bitcast(FP8X4),
-                    lhsT_scale=act_scales[src][:, m, k_cols],
+                    lhsT=act_codes[src][:, g, rows].bitcast(FP8X4),
+                    lhsT_scale=act_scales[src][:, g, rows],
                     rhs=w_words[(gate, src)][:, g, cols].bitcast(FP8X4),
                     rhs_scale=w_planes[gate][4 * n : P, cols],
                     start=(n == 0),
                     stop=(n == len(passes) - 1),
                 )
 
-        def add_bias(acc, half, gate, m, first_col, width):
-            cols = slice(half * N_TILE + first_col, half * N_TILE + first_col + width)
-            part = value[(half, gate, m)][:, first_col : first_col + width]
-            nc.vector.tensor_tensor(out=part, in0=acc[:], in1=bias_all[gate][:, cols], op=ALU.add)
+        def col_passes(acc, gate, d_tile):
+            channels = slice(d_tile * P, (d_tile + 1) * P)
+            for s, src, g in passes:
+                n = K_GROUPS * s + g
+                nc.tensor.matmul_mx(
+                    out=acc[:],
+                    lhsT=w_words[(gate, src)][:, g, channels].bitcast(FP8X4),
+                    lhsT_scale=w_planes[gate][4 * n : P, channels],
+                    rhs=act_codes[src][:, g, :].bitcast(FP8X4),
+                    rhs_scale=act_scales[src][:, g, :],
+                    start=(n == 0),
+                    stop=(n == len(passes) - 1),
+                )
 
-        def activate(half, gate, m, first_col, width):
-            part = value[(half, gate, m)][:, first_col : first_col + width]
-            nc.scalar.activation(out=part, in_=part, func=(ACT.Tanh if gate == "c" else ACT.Sigmoid))
-
-        def product(half, gate, m, engine):
-            out_gate = value[(half, gate, m)]
+        def finish_row_bank(acc, gate, half, m):
             cols = slice(half * N_TILE, (half + 1) * N_TILE)
-            if gate == "c":
-                engine.tensor_tensor(
-                    out=out_gate[:], in0=value[(half, "i", m)][:], in1=out_gate[:], op=ALU.mult
-                )
-            if gate == "f":
-                engine.tensor_tensor(
-                    out=out_gate[:], in0=out_gate[:], in1=c_sb[:, m, cols], op=ALU.mult
-                )
+            gate_sb = work.tile([P, N_TILE], F32, name="gate_" + gate, tag="gate_" + gate)
+            value[(gate, half, m)] = gate_sb
+            nc.vector.tensor_tensor(out=gate_sb[:], in0=acc[:], in1=bias_all[gate][:, cols], op=ALU.add)
+            nc.scalar.activation(out=gate_sb[:], in_=gate_sb[:], func=ACT.Sigmoid)
 
-        def new_gate_tile(half, gate, m):
-            out_gate = work.tile([P, N_TILE], F32, name="gate_" + gate, tag="gate_" + gate)
-            value[(half, gate, m)] = out_gate
+        def row_bank(gate, half, m):
+            acc = psum.tile([P, N_TILE], F32, name="acc", tag="bank")
+            row_passes(acc, gate, half, m, passes)
+            finish_row_bank(acc, gate, half, m)
 
-        def multiply_and_activate(step):
-            half, gate, m = banks[step]
-            if half == 0 and m == 0 and not BIAS_HEAD and BIAS_MODE == "pe":
-                spread_bias(gate)
-            new_gate_tile(half, gate, m)
-            if FIRST_SRC_MAJOR and step < ROW_TILES:
-                if step == 0:
-                    for mm in range(ROW_TILES):
-                        open_acc[mm] = psum.tile([P, N_TILE], F32, name="acc_first", tag="bank")
-                        multiply(open_acc[mm], half, gate, mm, 0, N_TILE, passes[:K_GROUPS])
-                acc = open_acc[m]
-                multiply(acc, half, gate, m, 0, N_TILE, passes[K_GROUPS:])
-            else:
-                acc = psum.tile([P, N_TILE], F32, tag="bank")
-                multiply(acc, half, gate, m, 0, N_TILE, passes)
-            add_bias(acc, half, gate, m, 0, N_TILE)
-            activate(half, gate, m, 0, N_TILE)
-            if gate == "c" and ENG_IC == "g":
-                product(half, gate, m, nc.gpsimd)
-            if gate == "f" and ENG_FC == "g":
-                product(half, gate, m, nc.gpsimd)
+        def col_bank(gate, half, j):
+            d_tile = half * D_TILES + j
+            acc = psum.tile([P, N_TILE], F32, name="acc", tag="bank")
+            col_passes(acc, gate, d_tile)
+            gate_sb = work.tile([P, N_TILE], F32, name="gate_" + gate, tag="gate_" + gate)
+            value[(gate, half, j)] = gate_sb
+            column = (HIDDEN // P) * COL_GATES.index(gate) + d_tile
+            nc.scalar.activation(
+                out=gate_sb[:],
+                in_=acc[:],
+                func=(ACT.Tanh if gate == "c" else ACT.Sigmoid),
+                bias=bias_cols[:, column : column + 1],
+            )
+
+        def times_c(half, m):
+            forget = value[("f", half, m)]
+            cols = slice(half * N_TILE, (half + 1) * N_TILE)
+            nc.vector.tensor_tensor(out=forget[:], in0=forget[:], in1=c_sb[:, m, cols], op=ALU.mult)
+
+        def input_product(half, j):
+            candidate = value[("c", half, j)]
+            nc.vector.tensor_tensor(
+                out=candidate[:], in0=value[("i", half, j)][:], in1=candidate[:], op=ALU.mult
+            )
+
+        def turn_products(half):
+            for m in range(ROW_TILES):
+                bank = psum.tile([P, D_TILES, P], F32, name="products", tag="bank")
+                product_bank[m] = bank
+                for j in range(D_TILES):
+                    nc.tensor.transpose(
+                        out=bank[:, j, :],
+                        in_=value[("c", half, j)][:, m * P : (m + 1) * P],
+                        identity=identity[:],
+                    )
 
         def finish_cell(half, m):
-            cell = value[(half, "c", m)]
-            nc.vector.tensor_tensor(out=cell[:], in0=cell[:], in1=value[(half, "f", m)][:], op=ALU.add)
+            cell = value[("f", half, m)]
+            products = product_bank[m][:].rearrange("p j d -> p (j d)")
+            nc.vector.tensor_tensor(out=cell[:], in0=products, in1=cell[:], op=ALU.add)
             nc.sync.dma_start(
                 out=out_1[m * P : (m + 1) * P, half * N_TILE : (half + 1) * N_TILE], in_=cell[:]
             )
-            cell_tanh = work.tile([P, N_TILE], F32, tag="cell_tanh")
-            value[(half, "t", m)] = cell_tanh
+            cell_tanh = work.tile([P, N_TILE], F32, name="cell_tanh", tag="cell_tanh")
+            value[("t", half, m)] = cell_tanh
             nc.scalar.activation(out=cell_tanh[:], in_=cell[:], func=ACT.Tanh)
 
-        def finish_hidden(half, m, engine, first_col, width):
-            part = slice(first_col, first_col + width)
-            hidden = value[(half, "o", m)]
-            engine.tensor_tensor(
-                out=hidden[:, part], in0=hidden[:, part], in1=value[(half, "t", m)][:, part], op=ALU.mult
+        def finish_hidden(half, m):
+            hidden = value[("o", half, m)]
+            nc.vector.tensor_tensor(
+                out=hidden[:], in0=hidden[:], in1=value[("t", half, m)][:], op=ALU.mult
             )
             nc.sync.dma_start(
-                out=out_0[m * P : (m + 1) * P, half * N_TILE + first_col : half * N_TILE + first_col + width],
-                in_=hidden[:, part],
+                out=out_0[m * P : (m + 1) * P, half * N_TILE : (half + 1) * N_TILE], in_=hidden[:]
             )
 
-        last = len(banks) - 1
-        for step in range(len(banks) + CELL_LAG):
-            if step < last:
-                half, gate, m = banks[step]
-                multiply_and_activate(step)
-                if gate == "o" and m % 2 == 0 and ENG_HO_EVEN == "g":
-                    finish_hidden(half, m, nc.gpsimd, 0, N_TILE)
-            if PROD_LAG <= step < len(banks) + PROD_LAG:
-                half, gate, m = banks[step - PROD_LAG]
-                if gate == "c" and ENG_IC == "v":
-                    product(half, gate, m, nc.vector)
-                if gate == "f" and ENG_FC == "v":
-                    product(half, gate, m, nc.vector)
-            if step >= CELL_LAG:
-                half, gate, m = banks[step - CELL_LAG]
-                if gate == "c":
-                    finish_cell(half, m)
-            if HIDDEN_LAG <= step < last + HIDDEN_LAG:
-                half, gate, m = banks[step - HIDDEN_LAG]
-                if gate == "o" and (m % 2 == 1 or ENG_HO_EVEN == "v"):
-                    finish_hidden(half, m, nc.vector, 0, N_TILE)
-            if step == last:
-                half, gate, m = banks[step]
-                new_gate_tile(half, gate, m)
-                starts = [sum(LAST_PIECES[:j]) for j in range(len(LAST_PIECES))]
-                for first_col, width in zip(starts, LAST_PIECES):
-                    piece = psum.tile([P, width], F32, name="piece", tag="bank")
-                    multiply(piece, half, gate, m, first_col, width, passes)
-                    add_bias(piece, half, gate, m, first_col, width)
-                    activate(half, gate, m, first_col, width)
-            if step == last + 1:
-                half, gate, m = banks[last]
-                starts = [sum(LAST_PIECES[:j]) for j in range(len(LAST_PIECES))]
-                for first_col, width in zip(starts, LAST_PIECES):
-                    finish_hidden(half, m, nc.vector, first_col, width)
+        for half in range(COL_HALVES):
+            if half == 0:
+                spread_bias("f")
+                first_banks = {}
+                for m in range(ROW_TILES):
+                    first_banks[m] = psum.tile([P, N_TILE], F32, name="acc_first", tag="bank")
+                    row_passes(first_banks[m], "f", 0, m, passes[:K_GROUPS])
+                for m in range(ROW_TILES):
+                    row_passes(first_banks[m], "f", 0, m, passes[K_GROUPS:])
+                    finish_row_bank(first_banks[m], "f", 0, m)
+                turn_bias_square()
+            else:
+                for m in range(ROW_TILES):
+                    row_bank("f", half, m)
+                    if m == 0:
+                        finish_hidden(half - 1, 0)
+                        finish_hidden(half - 1, 1)
+                    if m == 1:
+                        finish_hidden(half - 1, 2)
+                        finish_hidden(half - 1, 3)
+                    if m >= 2:
+                        times_c(half, m - 2)
+            for j in range(D_TILES):
+                col_bank("i", half, j)
+                if half == 0:
+                    times_c(0, j)
+                elif j < 2:
+                    times_c(half, j + 2)
+            for j in range(D_TILES):
+                col_bank("c", half, j)
+                if j > 0:
+                    input_product(half, j - 1)
+            input_product(half, D_TILES - 1)
+            if half == 0:
+                spread_bias("o")
+            row_bank("o", half, 0)
+            row_bank("o", half, 1)
+            turn_products(half)
+            finish_cell(half, 0)
+            finish_cell(half, 1)
+            row_bank("o", half, 2)
+            finish_cell(half, 2)
+            if half == COL_HALVES - 1:
+                finish_hidden(half, 0)
+            finish_cell(half, 3)
+            if half == COL_HALVES - 1:
+                finish_hidden(half, 1)
+            row_bank("o", half, 3)
+        finish_hidden(COL_HALVES - 1, 2)
+        finish_hidden(COL_HALVES - 1, 3)

@@ -28,6 +28,7 @@ SOURCES = ("x", "h")
 GATES = ("f", "i", "c", "o")
 ROW_GATES = ("f", "o")
 COL_GATES = ("i", "c")
+GATE_BUFS = {"f": 8, "i": 8, "c": 6, "o": 6}
 
 FLOPS = 2 * BATCH * (2 * FEATURES) * (4 * HIDDEN)
 
@@ -118,15 +119,12 @@ def tile_lstmcell_kernel(
                     in_=dram_bias[gate].rearrange("(j p) -> j p", p=P),
                 )
 
-        for gate in GATES:
-            load_bias(gate)
-
-        def load_scales(gate, src):
+        def load_scales(gate, src, queue=nc.sync, word=I32):
             for quad in range(QUADRANTS):
                 first = 32 * quad + 4 * K_GROUPS * SOURCES.index(src)
-                nc.sync.dma_start(
-                    out=w_planes[gate][first : first + 4 * K_GROUPS, :].bitcast(I32),
-                    in_=dram_scales[(gate, src)][:, 4 * quad : 4 * quad + 4, :].bitcast(I32),
+                queue.dma_start(
+                    out=w_planes[gate][first : first + 4 * K_GROUPS, :].bitcast(word),
+                    in_=dram_scales[(gate, src)][:, 4 * quad : 4 * quad + 4, :].bitcast(word),
                 )
 
         def load_words(gate, src, half):
@@ -141,6 +139,12 @@ def tile_lstmcell_kernel(
             tiles = slice(first, first + count)
             nc.sync.dma_start(out=raw[src][:, tiles, :], in_=by_tile[:, tiles, :])
 
+        load_scales("f", "h", nc.gpsimd, F32)
+        load_bias("f")
+        nc.gpsimd.dma_start(out=c_sb[:], in_=c.rearrange("(m p) d -> p m d", p=P))
+        for gate in ("i", "c", "o"):
+            load_bias(gate)
+
         load_activation("x", 0, 1)
         load_activation("x", 1, 1)
         load_scales("f", "x")
@@ -148,24 +152,24 @@ def tile_lstmcell_kernel(
         load_activation("h", 0, 2)
         load_activation("h", 2, 2)
         load_words("f", "x", 0)
-        load_scales("f", "h")
         load_words("f", "h", 0)
+        load_words("f", "x", 1)
         load_scales("i", "x")
-        load_words("i", "x", 0)
+        load_words("f", "h", 1)
         load_scales("i", "h")
+        load_words("i", "x", 0)
         load_words("i", "h", 0)
         load_scales("c", "x")
-        nc.sync.dma_start(out=c_sb[:], in_=c.rearrange("(m p) d -> p m d", p=P))
+        load_words("i", "x", 1)
         load_scales("c", "h")
+        load_words("i", "h", 1)
         load_words("c", "x", 0)
-        load_words("c", "h", 0)
         load_scales("o", "x")
-        load_words("o", "x", 0)
-        load_words("o", "h", 0)
+        load_words("c", "h", 0)
         load_scales("o", "h")
-        for gate in GATES:
+        for gate, half in (("o", 0), ("c", 1), ("o", 1)):
             for src in SOURCES:
-                load_words(gate, src, 1)
+                load_words(gate, src, half)
 
         def transpose_and_regroup(src, m):
             words = raw[src][:, m, :].bitcast(F32)
@@ -252,7 +256,7 @@ def tile_lstmcell_kernel(
 
         def finish_row_bank(acc, gate, half, m):
             cols = slice(half * N_TILE, (half + 1) * N_TILE)
-            gate_sb = work.tile([P, N_TILE], F32, name="gate_" + gate, tag="gate_" + gate)
+            gate_sb = work.tile([P, N_TILE], F32, name="gate_" + gate, tag="gate_" + gate, bufs=GATE_BUFS[gate])
             value[(gate, half, m)] = gate_sb
             nc.vector.tensor_tensor(out=gate_sb[:], in0=acc[:], in1=bias_all[gate][:, cols], op=ALU.add)
             nc.scalar.activation(out=gate_sb[:], in_=gate_sb[:], func=ACT.Sigmoid)
@@ -266,7 +270,7 @@ def tile_lstmcell_kernel(
             d_tile = half * D_TILES + j
             acc = psum.tile([P, N_TILE], F32, name="acc", tag="bank")
             col_passes(acc, gate, d_tile)
-            gate_sb = work.tile([P, N_TILE], F32, name="gate_" + gate, tag="gate_" + gate)
+            gate_sb = work.tile([P, N_TILE], F32, name="gate_" + gate, tag="gate_" + gate, bufs=GATE_BUFS[gate])
             value[(gate, half, j)] = gate_sb
             column = (HIDDEN // P) * COL_GATES.index(gate) + d_tile
             nc.scalar.activation(
@@ -318,38 +322,29 @@ def tile_lstmcell_kernel(
                 out=out_0[m * P : (m + 1) * P, half * N_TILE : (half + 1) * N_TILE], in_=hidden[:]
             )
 
+        spread_bias("f")
+        first_banks = {}
+        for m in range(ROW_TILES):
+            first_banks[m] = psum.tile([P, N_TILE], F32, name="acc_first", tag="bank")
+            row_passes(first_banks[m], "f", 0, m, passes[:K_GROUPS])
+        for m in range(ROW_TILES):
+            row_passes(first_banks[m], "f", 0, m, passes[K_GROUPS:])
+            finish_row_bank(first_banks[m], "f", 0, m)
+        for m in range(ROW_TILES):
+            row_bank("f", 1, m)
+        turn_bias_square()
         for half in range(COL_HALVES):
-            if half == 0:
-                spread_bias("f")
-                first_banks = {}
-                for m in range(ROW_TILES):
-                    first_banks[m] = psum.tile([P, N_TILE], F32, name="acc_first", tag="bank")
-                    row_passes(first_banks[m], "f", 0, m, passes[:K_GROUPS])
-                for m in range(ROW_TILES):
-                    row_passes(first_banks[m], "f", 0, m, passes[K_GROUPS:])
-                    finish_row_bank(first_banks[m], "f", 0, m)
-                turn_bias_square()
-            else:
-                for m in range(ROW_TILES):
-                    row_bank("f", half, m)
-                    if m == 0:
-                        finish_hidden(half - 1, 0)
-                        finish_hidden(half - 1, 1)
-                    if m == 1:
-                        finish_hidden(half - 1, 2)
-                        finish_hidden(half - 1, 3)
-                    if m >= 2:
-                        times_c(half, m - 2)
             for j in range(D_TILES):
                 col_bank("i", half, j)
-                if half == 0:
-                    times_c(0, j)
-                elif j < 2:
-                    times_c(half, j + 2)
+                times_c(half, j)
+        for half in range(COL_HALVES):
+            last = half == COL_HALVES - 1
             for j in range(D_TILES):
                 col_bank("c", half, j)
                 if j > 0:
                     input_product(half, j - 1)
+                if last:
+                    finish_hidden(half - 1, j)
             input_product(half, D_TILES - 1)
             if half == 0:
                 spread_bias("o")
@@ -360,10 +355,10 @@ def tile_lstmcell_kernel(
             finish_cell(half, 1)
             row_bank("o", half, 2)
             finish_cell(half, 2)
-            if half == COL_HALVES - 1:
+            if last:
                 finish_hidden(half, 0)
             finish_cell(half, 3)
-            if half == COL_HALVES - 1:
+            if last:
                 finish_hidden(half, 1)
             row_bank("o", half, 3)
         finish_hidden(COL_HALVES - 1, 2)

@@ -84,7 +84,10 @@ def tile_lstmcell_kernel(
                 )
         w_planes = {}
         for gate in GATES:
-            w_planes[gate] = keep.tile([P, HIDDEN], U8, name="planes_" + gate, align_bytes=64)
+            for src in SOURCES:
+                w_planes[(gate, src)] = keep.tile(
+                    [P, HIDDEN], U8, name="planes_" + src + gate, align_bytes=64
+                )
         bias_rows = {}
         bias_all = {}
         for gate in ROW_GATES:
@@ -99,7 +102,8 @@ def tile_lstmcell_kernel(
         table_warm = keep.tile([P, 1], F32)
 
         for gate in GATES:
-            nc.vector.memset(w_planes[gate][:].bitcast(I32), 0)
+            for src in SOURCES:
+                nc.vector.memset(w_planes[(gate, src)][:].bitcast(I32), 0)
         nc.vector.memset(bias_square[:].bitcast(I32), 0)
         for gate in ROW_GATES:
             nc.vector.memset(bias_rows[gate][:].bitcast(I32), 0)
@@ -121,9 +125,8 @@ def tile_lstmcell_kernel(
 
         def load_scales(gate, src, queue=nc.sync, word=I32):
             for quad in range(QUADRANTS):
-                first = 32 * quad + 4 * K_GROUPS * SOURCES.index(src)
                 queue.dma_start(
-                    out=w_planes[gate][first : first + 4 * K_GROUPS, :].bitcast(word),
+                    out=w_planes[(gate, src)][32 * quad : 32 * quad + 4 * K_GROUPS, :].bitcast(word),
                     in_=dram_scales[(gate, src)][:, 4 * quad : 4 * quad + 4, :].bitcast(word),
                 )
 
@@ -159,17 +162,19 @@ def tile_lstmcell_kernel(
         load_scales("i", "h")
         load_words("i", "x", 0)
         load_words("i", "h", 0)
-        load_scales("c", "x")
         load_words("i", "x", 1)
-        load_scales("c", "h")
+        load_scales("c", "x")
         load_words("i", "h", 1)
+        load_scales("c", "h")
         load_words("c", "x", 0)
-        load_scales("o", "x")
         load_words("c", "h", 0)
+        load_words("c", "x", 1)
+        load_scales("o", "x")
+        load_words("c", "h", 1)
         load_scales("o", "h")
-        for gate, half in (("o", 0), ("c", 1), ("o", 1)):
+        for half in range(COL_HALVES):
             for src in SOURCES:
-                load_words(gate, src, half)
+                load_words("o", src, half)
 
         def transpose_and_regroup(src, m):
             words = raw[src][:, m, :].bitcast(F32)
@@ -225,9 +230,9 @@ def tile_lstmcell_kernel(
         value = {}
         product_bank = {}
 
-        def row_passes(acc, gate, half, m, chosen):
+        def row_passes(acc, gate, half, m, chosen, first=0, width=N_TILE):
             rows = slice(m * P, (m + 1) * P)
-            cols = slice(half * N_TILE, (half + 1) * N_TILE)
+            cols = slice(half * N_TILE + first, half * N_TILE + first + width)
             for s, src, g in chosen:
                 n = K_GROUPS * s + g
                 nc.tensor.matmul_mx(
@@ -235,7 +240,7 @@ def tile_lstmcell_kernel(
                     lhsT=act_codes[src][:, g, rows].bitcast(FP8X4),
                     lhsT_scale=act_scales[src][:, g, rows],
                     rhs=w_words[(gate, src)][:, g, cols].bitcast(FP8X4),
-                    rhs_scale=w_planes[gate][4 * n : P, cols],
+                    rhs_scale=w_planes[(gate, src)][4 * g : P, cols],
                     start=(n == 0),
                     stop=(n == len(passes) - 1),
                 )
@@ -247,24 +252,27 @@ def tile_lstmcell_kernel(
                 nc.tensor.matmul_mx(
                     out=acc[:],
                     lhsT=w_words[(gate, src)][:, g, channels].bitcast(FP8X4),
-                    lhsT_scale=w_planes[gate][4 * n : P, channels],
+                    lhsT_scale=w_planes[(gate, src)][4 * g : P, channels],
                     rhs=act_codes[src][:, g, :].bitcast(FP8X4),
                     rhs_scale=act_scales[src][:, g, :],
                     start=(n == 0),
                     stop=(n == len(passes) - 1),
                 )
 
-        def finish_row_bank(acc, gate, half, m):
-            cols = slice(half * N_TILE, (half + 1) * N_TILE)
-            gate_sb = work.tile([P, N_TILE], F32, name="gate_" + gate, tag="gate_" + gate, bufs=GATE_BUFS[gate])
-            value[(gate, half, m)] = gate_sb
-            nc.vector.tensor_tensor(out=gate_sb[:], in0=acc[:], in1=bias_all[gate][:, cols], op=ALU.add)
-            nc.scalar.activation(out=gate_sb[:], in_=gate_sb[:], func=ACT.Sigmoid)
+        def finish_row_bank(acc, gate, half, m, first=0, width=N_TILE):
+            cols = slice(half * N_TILE + first, half * N_TILE + first + width)
+            if first == 0:
+                value[(gate, half, m)] = work.tile(
+                    [P, N_TILE], F32, name="gate_" + gate, tag="gate_" + gate, bufs=GATE_BUFS[gate]
+                )
+            part = value[(gate, half, m)][:, first : first + width]
+            nc.vector.tensor_tensor(out=part, in0=acc[:], in1=bias_all[gate][:, cols], op=ALU.add)
+            nc.scalar.activation(out=part, in_=part, func=ACT.Sigmoid)
 
-        def row_bank(gate, half, m):
-            acc = psum.tile([P, N_TILE], F32, name="acc", tag="bank")
-            row_passes(acc, gate, half, m, passes)
-            finish_row_bank(acc, gate, half, m)
+        def row_bank(gate, half, m, first=0, width=N_TILE):
+            acc = psum.tile([P, width], F32, name="acc", tag="bank")
+            row_passes(acc, gate, half, m, passes, first, width)
+            finish_row_bank(acc, gate, half, m, first, width)
 
         def col_bank(gate, half, j):
             d_tile = half * D_TILES + j
@@ -313,20 +321,20 @@ def tile_lstmcell_kernel(
             value[("t", half, m)] = cell_tanh
             nc.scalar.activation(out=cell_tanh[:], in_=cell[:], func=ACT.Tanh)
 
-        def finish_hidden(half, m):
+        def finish_hidden(half, m, engine, first=0, width=N_TILE):
+            part = slice(first, first + width)
+            cols = slice(half * N_TILE + first, half * N_TILE + first + width)
             hidden = value[("o", half, m)]
-            nc.vector.tensor_tensor(
-                out=hidden[:], in0=hidden[:], in1=value[("t", half, m)][:], op=ALU.mult
+            engine.tensor_tensor(
+                out=hidden[:, part], in0=hidden[:, part], in1=value[("t", half, m)][:, part], op=ALU.mult
             )
-            nc.sync.dma_start(
-                out=out_0[m * P : (m + 1) * P, half * N_TILE : (half + 1) * N_TILE], in_=hidden[:]
-            )
+            nc.sync.dma_start(out=out_0[m * P : (m + 1) * P, cols], in_=hidden[:, part])
 
-        spread_bias("f")
         first_banks = {}
         for m in range(ROW_TILES):
             first_banks[m] = psum.tile([P, N_TILE], F32, name="acc_first", tag="bank")
             row_passes(first_banks[m], "f", 0, m, passes[:K_GROUPS])
+        spread_bias("f")
         for m in range(ROW_TILES):
             row_passes(first_banks[m], "f", 0, m, passes[K_GROUPS:])
             finish_row_bank(first_banks[m], "f", 0, m)
@@ -337,29 +345,47 @@ def tile_lstmcell_kernel(
             for j in range(D_TILES):
                 col_bank("i", half, j)
                 times_c(half, j)
-        for half in range(COL_HALVES):
-            last = half == COL_HALVES - 1
-            for j in range(D_TILES):
-                col_bank("c", half, j)
-                if j > 0:
-                    input_product(half, j - 1)
-                if last:
-                    finish_hidden(half - 1, j)
-            input_product(half, D_TILES - 1)
-            if half == 0:
-                spread_bias("o")
-            row_bank("o", half, 0)
-            row_bank("o", half, 1)
-            turn_products(half)
-            finish_cell(half, 0)
-            finish_cell(half, 1)
-            row_bank("o", half, 2)
-            finish_cell(half, 2)
-            if last:
-                finish_hidden(half, 0)
-            finish_cell(half, 3)
-            if last:
-                finish_hidden(half, 1)
-            row_bank("o", half, 3)
-        finish_hidden(COL_HALVES - 1, 2)
-        finish_hidden(COL_HALVES - 1, 3)
+
+        col_bank("c", 0, 0)
+        for j in range(1, D_TILES):
+            col_bank("c", 0, j)
+            input_product(0, j - 1)
+        col_bank("c", 1, 0)
+        input_product(0, 3)
+        col_bank("c", 1, 1)
+        input_product(1, 0)
+        turn_products(0)
+        finish_cell(0, 0)
+        col_bank("c", 1, 2)
+        input_product(1, 1)
+        finish_cell(0, 1)
+        finish_cell(0, 2)
+        col_bank("c", 1, 3)
+        input_product(1, 2)
+        finish_cell(0, 3)
+        input_product(1, 3)
+        spread_bias("o")
+        row_bank("o", 0, 0)
+        row_bank("o", 0, 1)
+        turn_products(1)
+        finish_hidden(0, 0, nc.gpsimd)
+        finish_cell(1, 0)
+        finish_cell(1, 1)
+        row_bank("o", 0, 2)
+        finish_hidden(0, 1, nc.gpsimd)
+        finish_cell(1, 2)
+        row_bank("o", 0, 3)
+        finish_hidden(0, 2, nc.gpsimd)
+        finish_cell(1, 3)
+        row_bank("o", 1, 0)
+        finish_hidden(0, 3, nc.gpsimd)
+        row_bank("o", 1, 1)
+        finish_hidden(1, 0, nc.vector)
+        row_bank("o", 1, 2)
+        finish_hidden(1, 1, nc.vector)
+        piece = N_TILE // 2
+        row_bank("o", 1, 3, 0, piece)
+        finish_hidden(1, 2, nc.vector)
+        row_bank("o", 1, 3, piece, piece)
+        finish_hidden(1, 3, nc.vector, 0, piece)
+        finish_hidden(1, 3, nc.vector, piece, piece)

@@ -26,9 +26,8 @@ D_TILES = N_TILE // P
 QUADRANTS = 4
 SOURCES = ("x", "h")
 GATES = ("f", "i", "c", "o")
-ROW_GATES = ("f", "o")
-COL_GATES = ("i", "c")
-GATE_BUFS = {"f": 8, "i": 8, "c": 6, "o": 6}
+ROW_BANKS = (("f", 0), ("f", 1), ("i", 0), ("c", 0), ("o", 0), ("o", 1))
+GATE_BUFS = {"f": 8, "i": 8, "c": 6, "o": 8}
 
 FLOPS = 2 * BATCH * (2 * FEATURES) * (4 * HIDDEN)
 
@@ -90,9 +89,10 @@ def tile_lstmcell_kernel(
                 )
         bias_rows = {}
         bias_all = {}
-        for gate in ROW_GATES:
-            bias_rows[gate] = keep.tile([P, HIDDEN], BF16, name="bias_rows_" + gate)
-            bias_all[gate] = keep.tile([P, HIDDEN], BF16, name="bias_all_" + gate)
+        for gate in GATES:
+            if (gate, 0) in ROW_BANKS:
+                bias_rows[gate] = keep.tile([P, HIDDEN], BF16, name="bias_rows_" + gate)
+                bias_all[gate] = keep.tile([P, HIDDEN], BF16, name="bias_all_" + gate)
         bias_square = keep.tile([P, P], BF16, name="bias_square")
         bias_cols = keep.tile([P, P], F32, name="bias_cols")
         c_sb = keep.tile([P, ROW_TILES, HIDDEN], BF16)
@@ -105,7 +105,7 @@ def tile_lstmcell_kernel(
             for src in SOURCES:
                 nc.vector.memset(w_planes[(gate, src)][:].bitcast(I32), 0)
         nc.vector.memset(bias_square[:].bitcast(I32), 0)
-        for gate in ROW_GATES:
+        for gate in bias_rows:
             nc.vector.memset(bias_rows[gate][:].bitcast(I32), 0)
         nc.vector.memset(ones[:], 1.0)
         nc.vector.memset(table_warm[:], 0.0)
@@ -114,10 +114,10 @@ def tile_lstmcell_kernel(
         nc.vector.tensor_copy(out=identity_bf[:], in_=identity[:])
 
         def load_bias(gate):
-            if gate in ROW_GATES:
+            if gate in bias_rows:
                 nc.gpsimd.dma_start(out=bias_rows[gate][0:1, :], in_=dram_bias[gate].unsqueeze(0))
-            else:
-                first = (HIDDEN // P) * COL_GATES.index(gate)
+            if (gate, 1) not in ROW_BANKS:
+                first = (HIDDEN // P) * GATES.index(gate)
                 nc.gpsimd.dma_start(
                     out=bias_square[first : first + HIDDEN // P, :],
                     in_=dram_bias[gate].rearrange("(j p) -> j p", p=P),
@@ -143,24 +143,23 @@ def tile_lstmcell_kernel(
             nc.sync.dma_start(out=raw[src][:, tiles, :], in_=by_tile[:, tiles, :])
 
         load_scales("f", "h", nc.gpsimd, F32)
-        load_bias("f")
-        nc.gpsimd.dma_start(out=c_sb[:], in_=c.rearrange("(m p) d -> p m d", p=P))
-        for gate in ("i", "c", "o"):
+        for gate in ("f", "i", "c", "o"):
             load_bias(gate)
+        nc.gpsimd.dma_start(out=c_sb[:], in_=c.rearrange("(m p) d -> p m d", p=P))
 
         load_activation("x", 0, 1)
         load_activation("x", 1, 1)
-        load_scales("f", "x")
         load_activation("x", 2, 2)
         load_activation("h", 0, 2)
+        load_scales("f", "x")
         load_activation("h", 2, 2)
         load_words("f", "x", 0)
         load_words("f", "h", 0)
         load_words("f", "x", 1)
-        load_scales("i", "x")
         load_words("f", "h", 1)
-        load_scales("i", "h")
+        load_scales("i", "x")
         load_words("i", "x", 0)
+        load_scales("i", "h")
         load_words("i", "h", 0)
         load_words("i", "x", 1)
         load_scales("c", "x")
@@ -172,9 +171,10 @@ def tile_lstmcell_kernel(
         load_scales("o", "x")
         load_words("c", "h", 1)
         load_scales("o", "h")
-        for half in range(COL_HALVES):
-            for src in SOURCES:
-                load_words("o", src, half)
+        load_words("o", "x", 0)
+        load_words("o", "h", 0)
+        load_words("o", "x", 1)
+        load_words("o", "h", 1)
 
         def transpose_and_regroup(src, m):
             words = raw[src][:, m, :].bitcast(F32)
@@ -205,12 +205,14 @@ def tile_lstmcell_kernel(
 
         def spread_bias(gate):
             spread = psum.tile([P, HIDDEN], BF16, name="spread", tag="bank")
-            for half in range(COL_HALVES):
+            halves = [half for half in range(COL_HALVES) if (gate, half) in ROW_BANKS]
+            for half in halves:
                 cols = slice(half * N_TILE, (half + 1) * N_TILE)
                 nc.tensor.matmul(
                     out=spread[:, cols], lhsT=ones[:], rhs=bias_rows[gate][:, cols], start=True, stop=True
                 )
-            nc.scalar.copy(out=bias_all[gate][:], in_=spread[:])
+            used = slice(0, len(halves) * N_TILE)
+            nc.scalar.copy(out=bias_all[gate][:, used], in_=spread[:, used])
 
         def turn_bias_square():
             turned = psum.tile([P, P], BF16, name="turned", tag="bank")
@@ -267,7 +269,7 @@ def tile_lstmcell_kernel(
                 )
             part = value[(gate, half, m)][:, first : first + width]
             nc.vector.tensor_tensor(out=part, in0=acc[:], in1=bias_all[gate][:, cols], op=ALU.add)
-            nc.scalar.activation(out=part, in_=part, func=ACT.Sigmoid)
+            nc.scalar.activation(out=part, in_=part, func=(ACT.Tanh if gate == "c" else ACT.Sigmoid))
 
         def row_bank(gate, half, m, first=0, width=N_TILE):
             acc = psum.tile([P, width], F32, name="acc", tag="bank")
@@ -280,7 +282,7 @@ def tile_lstmcell_kernel(
             col_passes(acc, gate, d_tile)
             gate_sb = work.tile([P, N_TILE], F32, name="gate_" + gate, tag="gate_" + gate, bufs=GATE_BUFS[gate])
             value[(gate, half, j)] = gate_sb
-            column = (HIDDEN // P) * COL_GATES.index(gate) + d_tile
+            column = (HIDDEN // P) * GATES.index(gate) + d_tile
             nc.scalar.activation(
                 out=gate_sb[:],
                 in_=acc[:],
@@ -288,14 +290,14 @@ def tile_lstmcell_kernel(
                 bias=bias_cols[:, column : column + 1],
             )
 
-        def times_c(half, m):
+        def times_c(half, m, engine):
             forget = value[("f", half, m)]
             cols = slice(half * N_TILE, (half + 1) * N_TILE)
-            nc.vector.tensor_tensor(out=forget[:], in0=forget[:], in1=c_sb[:, m, cols], op=ALU.mult)
+            engine.tensor_tensor(out=forget[:], in0=forget[:], in1=c_sb[:, m, cols], op=ALU.mult)
 
-        def input_product(half, j):
+        def input_product(half, j, engine):
             candidate = value[("c", half, j)]
-            nc.vector.tensor_tensor(
+            engine.tensor_tensor(
                 out=candidate[:], in0=value[("i", half, j)][:], in1=candidate[:], op=ALU.mult
             )
 
@@ -312,7 +314,10 @@ def tile_lstmcell_kernel(
 
         def finish_cell(half, m):
             cell = value[("f", half, m)]
-            products = product_bank[m][:].rearrange("p j d -> p (j d)")
+            if ("c", half) in ROW_BANKS:
+                products = value[("c", half, m)][:]
+            else:
+                products = product_bank[m][:].rearrange("p j d -> p (j d)")
             nc.vector.tensor_tensor(out=cell[:], in0=products, in1=cell[:], op=ALU.add)
             nc.sync.dma_start(
                 out=out_1[m * P : (m + 1) * P, half * N_TILE : (half + 1) * N_TILE], in_=cell[:]
@@ -334,58 +339,56 @@ def tile_lstmcell_kernel(
         for m in range(ROW_TILES):
             first_banks[m] = psum.tile([P, N_TILE], F32, name="acc_first", tag="bank")
             row_passes(first_banks[m], "f", 0, m, passes[:K_GROUPS])
-        spread_bias("f")
-        for m in range(ROW_TILES):
-            row_passes(first_banks[m], "f", 0, m, passes[K_GROUPS:])
-            finish_row_bank(first_banks[m], "f", 0, m)
-        for m in range(ROW_TILES):
-            row_bank("f", 1, m)
-        turn_bias_square()
-        for half in range(COL_HALVES):
-            for j in range(D_TILES):
-                col_bank("i", half, j)
-                times_c(half, j)
+        later = []
 
-        col_bank("c", 0, 0)
-        for j in range(1, D_TILES):
-            col_bank("c", 0, j)
-            input_product(0, j - 1)
-        col_bank("c", 1, 0)
-        input_product(0, 3)
-        col_bank("c", 1, 1)
-        input_product(1, 0)
-        turn_products(0)
-        finish_cell(0, 0)
-        col_bank("c", 1, 2)
-        input_product(1, 1)
-        finish_cell(0, 1)
-        finish_cell(0, 2)
-        col_bank("c", 1, 3)
-        input_product(1, 2)
-        finish_cell(0, 3)
-        input_product(1, 3)
-        spread_bias("o")
-        row_bank("o", 0, 0)
-        row_bank("o", 0, 1)
-        turn_products(1)
-        finish_hidden(0, 0, nc.gpsimd)
-        finish_cell(1, 0)
-        finish_cell(1, 1)
-        row_bank("o", 0, 2)
-        finish_hidden(0, 1, nc.gpsimd)
-        finish_cell(1, 2)
-        row_bank("o", 0, 3)
-        finish_hidden(0, 2, nc.gpsimd)
-        finish_cell(1, 3)
-        row_bank("o", 1, 0)
-        finish_hidden(0, 3, nc.gpsimd)
-        row_bank("o", 1, 1)
-        finish_hidden(1, 0, nc.vector)
-        row_bank("o", 1, 2)
-        finish_hidden(1, 1, nc.vector)
-        piece = N_TILE // 2
-        row_bank("o", 1, 3, 0, piece)
-        finish_hidden(1, 2, nc.vector)
-        row_bank("o", 1, 3, piece, piece)
-        finish_hidden(1, 3, nc.vector, 0, piece)
-        finish_hidden(1, 3, nc.vector, piece, piece)
+        def emit(now):
+            for due in sorted(set(d for d, w in later if d <= now)):
+                for d, w in [x for x in later if x[0] == due]:
+                    w()
+            later[:] = [x for x in later if x[0] > now]
+
+        n = 0
+        for gate, half in (("f", 0), ("f", 1), ("i", 0), ("i", 1), ("c", 0), ("c", 1), ("o", 0), ("o", 1)):
+            for m in range(ROW_TILES):
+                if True:
+                    step = n
+                    n += 1
+                    emit(step - 0.5)
+                    if step < ROW_TILES:
+                        row_passes(first_banks[m], "f", 0, m, passes[K_GROUPS:])
+                        if m == 1:
+                            spread_bias("f")
+                            finish_row_bank(first_banks[0], "f", 0, 0)
+                        if m > 0:
+                            finish_row_bank(first_banks[m], "f", 0, m)
+                    elif step == 4 * ROW_TILES * COL_HALVES - 1:
+                        piece = N_TILE // 2
+                        row_bank("o", 1, 3, 0, piece)
+                        row_bank("o", 1, 3, piece, piece)
+                    elif (gate, half) in ROW_BANKS:
+                        row_bank(gate, half, m)
+                    else:
+                        col_bank(gate, half, m)
+                    if step == 7:
+                        spread_bias("i")
+                        spread_bias("c")
+                        turn_bias_square()
+                        spread_bias("o")
+                    if gate == ("i"):
+                        later.append((step + 0, lambda half=half, m=m: times_c(half, m, nc.vector)))
+                    if gate == "c" and (gate, half) not in ROW_BANKS:
+                        later.append((step + 0.5, lambda half=half, m=m: input_product(half, m, nc.vector)))
+                        if m == 3:
+                            later.append((step + 3, lambda half=half: turn_products(half)))
+                            for mm, lag in enumerate((3, 3, 3, 4)):
+                                later.append((step + lag, lambda half=half, mm=mm: finish_cell(half, mm)))
+                    if gate == "c" and (gate, half) in ROW_BANKS:
+                        later.append((step + 1, lambda half=half, m=m: input_product(half, m, nc.vector)))
+                        later.append((step + 2, lambda half=half, m=m: finish_cell(half, m)))
+                    if gate == "o" and step < 31:
+                        later.append((step + (half == 0 and 0 or 1), lambda half=half, m=m: finish_hidden(half, m, nc.gpsimd if half == 0 else nc.vector)))
+                    if step == 31:
+                        later.append((step + 2, lambda: finish_hidden(1, 3, nc.vector, 0, N_TILE // 2)))
+                        later.append((step + 2, lambda: finish_hidden(1, 3, nc.vector, N_TILE // 2, N_TILE // 2)))
+                    emit(step)
+        emit(1000)

@@ -29,6 +29,8 @@ GATES = ("f", "i", "c", "o")
 ROW_BANKS = (("f", 0), ("f", 1), ("i", 0), ("c", 0), ("o", 0), ("o", 1))
 GATE_BUFS = {"f": 8, "i": 8, "c": 6, "o": 8}
 
+HEAD_BIASES = {("x", 1): "f", ("x", 3): "i", ("h", 0): "c", ("h", 1): "o"}
+
 FLOPS = 2 * BATCH * (2 * FEATURES) * (4 * HIDDEN)
 
 
@@ -85,7 +87,7 @@ def tile_lstmcell_kernel(
         for gate in GATES:
             for src in SOURCES:
                 w_planes[(gate, src)] = keep.tile(
-                    [P, HIDDEN], U8, name="planes_" + src + gate, align_bytes=64
+                    [P, K_GROUPS, HIDDEN], U8, name="planes_" + src + gate, align_bytes=64
                 )
         bias_rows = {}
         bias_all = {}
@@ -101,22 +103,23 @@ def tile_lstmcell_kernel(
         identity_bf = keep.tile([P, P], BF16)
         table_warm = keep.tile([P, 1], F32)
 
-        for gate in GATES:
-            for src in SOURCES:
-                nc.vector.memset(w_planes[(gate, src)][:].bitcast(I32), 0)
-        nc.vector.memset(bias_square[:].bitcast(I32), 0)
         for gate in bias_rows:
             nc.vector.memset(bias_rows[gate][:].bitcast(I32), 0)
         nc.vector.memset(ones[:], 1.0)
+        for gate in GATES:
+            for src in SOURCES:
+                nc.vector.memset(w_planes[(gate, src)][:].rearrange("p g n -> p (g n)").bitcast(I32), 0)
+        nc.vector.memset(bias_square[:].bitcast(I32), 0)
         nc.vector.memset(table_warm[:], 0.0)
         nc.scalar.activation(out=table_warm[:], in_=table_warm[:], func=ACT.Sigmoid)
         make_identity(nc, identity[:])
         nc.vector.tensor_copy(out=identity_bf[:], in_=identity[:])
 
-        def load_bias(gate):
-            if gate in bias_rows:
-                nc.gpsimd.dma_start(out=bias_rows[gate][0:1, :], in_=dram_bias[gate].unsqueeze(0))
-            if (gate, 1) not in ROW_BANKS:
+        def load_bias_row(gate):
+            nc.sync.dma_start(out=bias_rows[gate][0:1, :], in_=dram_bias[gate].unsqueeze(0))
+
+        def load_bias_column(gate):
+            if True:
                 first = (HIDDEN // P) * GATES.index(gate)
                 nc.gpsimd.dma_start(
                     out=bias_square[first : first + HIDDEN // P, :],
@@ -126,54 +129,61 @@ def tile_lstmcell_kernel(
         def load_scales(gate, src, queue=nc.sync, word=I32):
             for quad in range(QUADRANTS):
                 queue.dma_start(
-                    out=w_planes[(gate, src)][32 * quad : 32 * quad + 4 * K_GROUPS, :].bitcast(word),
-                    in_=dram_scales[(gate, src)][:, 4 * quad : 4 * quad + 4, :].bitcast(word),
+                    out=w_planes[(gate, src)][32 * quad : 32 * quad + 4, :, :].bitcast(word),
+                    in_=dram_scales[(gate, src)].rearrange("g q n -> q g n")[4 * quad : 4 * quad + 4, :, :].bitcast(word),
                 )
 
-        def load_words(gate, src, half):
-            cols = slice(half * N_TILE, (half + 1) * N_TILE)
-            words = dram_words[(gate, src)].rearrange("g p n t -> p g (n t)").bitcast(I32)
-            nc.sync.dma_start(
-                out=w_words[(gate, src)][:, :, cols].bitcast(I32), in_=words[:, :, cols]
-            )
+        def load_words(gate, src, g):
+            words = dram_words[(gate, src)].rearrange("g p n t -> g p (n t)").bitcast(I32)
+            nc.sync.dma_start(out=w_words[(gate, src)][:, g, :].bitcast(I32), in_=words[g])
 
         def load_activation(src, first, count):
-            by_tile = activations[src].rearrange("(m p) k -> p m k", p=P)
-            tiles = slice(first, first + count)
-            nc.sync.dma_start(out=raw[src][:, tiles, :], in_=by_tile[:, tiles, :])
+            by_partition = activations[src].rearrange("(p m) k -> p (m k)", m=ROW_TILES)
+            tiles = slice(first * FEATURES, (first + count) * FEATURES)
+            side_by_side = raw[src][:].rearrange("p m k -> p (m k)")
+            nc.sync.dma_start(out=side_by_side[:, tiles], in_=by_partition[:, tiles])
+
+        def load_cell():
+            nc.sync.dma_start(
+                out=c_sb[:].rearrange("p m d -> p (m d)"),
+                in_=c.rearrange("(p m) d -> p (m d)", m=ROW_TILES),
+            )
 
         load_scales("f", "h", nc.gpsimd, F32)
-        for gate in ("f", "i", "c", "o"):
-            load_bias(gate)
-        nc.gpsimd.dma_start(out=c_sb[:], in_=c.rearrange("(m p) d -> p m d", p=P))
+        for gate in ("i", "c"):
+            load_bias_column(gate)
 
-        load_activation("x", 0, 1)
-        load_activation("x", 1, 1)
+        load_activation("x", 0, 2)
+        load_bias_row("f")
+        load_bias_row("i")
+        load_bias_row("c")
+        load_bias_row("o")
         load_activation("x", 2, 2)
         load_activation("h", 0, 2)
-        load_scales("f", "x")
         load_activation("h", 2, 2)
+        load_scales("f", "x")
         load_words("f", "x", 0)
-        load_words("f", "h", 0)
         load_words("f", "x", 1)
+        load_words("f", "h", 0)
         load_words("f", "h", 1)
         load_scales("i", "x")
         load_words("i", "x", 0)
+        load_words("i", "x", 1)
         load_scales("i", "h")
         load_words("i", "h", 0)
-        load_words("i", "x", 1)
-        load_scales("c", "x")
         load_words("i", "h", 1)
-        load_scales("c", "h")
+        load_cell()
+        load_scales("c", "x")
         load_words("c", "x", 0)
-        load_words("c", "h", 0)
         load_words("c", "x", 1)
-        load_scales("o", "x")
+        load_scales("c", "h")
+        load_words("c", "h", 0)
         load_words("c", "h", 1)
-        load_scales("o", "h")
+        load_scales("o", "x")
         load_words("o", "x", 0)
-        load_words("o", "h", 0)
         load_words("o", "x", 1)
+        load_scales("o", "h")
+        load_words("o", "h", 0)
         load_words("o", "h", 1)
 
         def transpose_and_regroup(src, m):
@@ -222,6 +232,8 @@ def tile_lstmcell_kernel(
         for src in SOURCES:
             for m in range(ROW_TILES):
                 transpose_and_regroup(src, m)
+                if (src, m) in HEAD_BIASES:
+                    spread_bias(HEAD_BIASES[(src, m)])
                 if m == 2:
                     quantise(src, 0, 2)
                 if m == 0 and src == "h":
@@ -242,7 +254,7 @@ def tile_lstmcell_kernel(
                     lhsT=act_codes[src][:, g, rows].bitcast(FP8X4),
                     lhsT_scale=act_scales[src][:, g, rows],
                     rhs=w_words[(gate, src)][:, g, cols].bitcast(FP8X4),
-                    rhs_scale=w_planes[(gate, src)][4 * g : P, cols],
+                    rhs_scale=w_planes[(gate, src)][:, g, cols],
                     start=(n == 0),
                     stop=(n == len(passes) - 1),
                 )
@@ -254,7 +266,7 @@ def tile_lstmcell_kernel(
                 nc.tensor.matmul_mx(
                     out=acc[:],
                     lhsT=w_words[(gate, src)][:, g, channels].bitcast(FP8X4),
-                    lhsT_scale=w_planes[(gate, src)][4 * g : P, channels],
+                    lhsT_scale=w_planes[(gate, src)][:, g, channels],
                     rhs=act_codes[src][:, g, :].bitcast(FP8X4),
                     rhs_scale=act_scales[src][:, g, :],
                     start=(n == 0),
@@ -312,6 +324,9 @@ def tile_lstmcell_kernel(
                         identity=identity[:],
                     )
 
+        def by_row_tile(out):
+            return out.rearrange("(p m) d -> p m d", m=ROW_TILES)
+
         def finish_cell(half, m):
             cell = value[("f", half, m)]
             if ("c", half) in ROW_BANKS:
@@ -320,7 +335,7 @@ def tile_lstmcell_kernel(
                 products = product_bank[m][:].rearrange("p j d -> p (j d)")
             nc.vector.tensor_tensor(out=cell[:], in0=products, in1=cell[:], op=ALU.add)
             nc.sync.dma_start(
-                out=out_1[m * P : (m + 1) * P, half * N_TILE : (half + 1) * N_TILE], in_=cell[:]
+                out=by_row_tile(out_1)[:, m, half * N_TILE : (half + 1) * N_TILE], in_=cell[:]
             )
             cell_tanh = work.tile([P, N_TILE], F32, name="cell_tanh", tag="cell_tanh")
             value[("t", half, m)] = cell_tanh
@@ -333,12 +348,17 @@ def tile_lstmcell_kernel(
             engine.tensor_tensor(
                 out=hidden[:, part], in0=hidden[:, part], in1=value[("t", half, m)][:, part], op=ALU.mult
             )
-            nc.sync.dma_start(out=out_0[m * P : (m + 1) * P, cols], in_=hidden[:, part])
+            nc.sync.dma_start(out=by_row_tile(out_0)[:, m, cols], in_=hidden[:, part])
 
         first_banks = {}
-        for m in range(ROW_TILES):
-            first_banks[m] = psum.tile([P, N_TILE], F32, name="acc_first", tag="bank")
-            row_passes(first_banks[m], "f", 0, m, passes[:K_GROUPS])
+        for half in range(COL_HALVES):
+            for m in range(ROW_TILES):
+                first_banks[(half, m)] = psum.tile([P, N_TILE], F32, name="acc_first", tag="bank")
+                row_passes(first_banks[(half, m)], "f", half, m, passes[:1])
+        for chosen in passes[1:-1]:
+            for half in range(COL_HALVES):
+                for m in range(ROW_TILES):
+                    row_passes(first_banks[(half, m)], "f", half, m, [chosen])
         later = []
 
         def emit(now):
@@ -354,13 +374,9 @@ def tile_lstmcell_kernel(
                     step = n
                     n += 1
                     emit(step - 0.5)
-                    if step < ROW_TILES:
-                        row_passes(first_banks[m], "f", 0, m, passes[K_GROUPS:])
-                        if m == 1:
-                            spread_bias("f")
-                            finish_row_bank(first_banks[0], "f", 0, 0)
-                        if m > 0:
-                            finish_row_bank(first_banks[m], "f", 0, m)
+                    if gate == "f":
+                        row_passes(first_banks[(half, m)], "f", half, m, passes[-1:])
+                        finish_row_bank(first_banks[(half, m)], "f", half, m)
                     elif step == 4 * ROW_TILES * COL_HALVES - 1:
                         piece = N_TILE // 2
                         row_bank("o", 1, 3, 0, piece)
@@ -369,11 +385,8 @@ def tile_lstmcell_kernel(
                         row_bank(gate, half, m)
                     else:
                         col_bank(gate, half, m)
-                    if step == 7:
-                        spread_bias("i")
-                        spread_bias("c")
+                    if step == 11:
                         turn_bias_square()
-                        spread_bias("o")
                     if gate == ("i"):
                         later.append((step + 0, lambda half=half, m=m: times_c(half, m, nc.vector)))
                     if gate == "c" and (gate, half) not in ROW_BANKS:

@@ -29,7 +29,7 @@ GATES = ("f", "i", "c", "o")
 ROW_BANKS = (("f", 0), ("f", 1), ("i", 0), ("c", 0), ("o", 0), ("o", 1))
 GATE_BUFS = {"f": 8, "i": 8, "c": 6, "o": 8}
 
-HEAD_BIASES = {("x", 1): "f", ("x", 3): "i", ("h", 0): "c", ("h", 1): "o"}
+HEAD_BIASES = {("x", 0): "f", ("x", 1): "i", ("x", 3): "c", ("h", 1): "o"}
 
 FLOPS = 2 * BATCH * (2 * FEATURES) * (4 * HIDDEN)
 
@@ -89,34 +89,32 @@ def tile_lstmcell_kernel(
                 w_planes[(gate, src)] = keep.tile(
                     [P, K_GROUPS, HIDDEN], U8, name="planes_" + src + gate, align_bytes=64
                 )
-        bias_rows = {}
+        bias_rows = keep.tile([P, HIDDEN], BF16)
         bias_all = {}
         for gate in GATES:
-            if (gate, 0) in ROW_BANKS:
-                bias_rows[gate] = keep.tile([P, HIDDEN], BF16, name="bias_rows_" + gate)
-                bias_all[gate] = keep.tile([P, HIDDEN], BF16, name="bias_all_" + gate)
+            bias_all[gate] = keep.tile([P, HIDDEN], BF16, name="bias_all_" + gate)
         bias_square = keep.tile([P, P], BF16, name="bias_square")
         bias_cols = keep.tile([P, P], F32, name="bias_cols")
         c_sb = keep.tile([P, ROW_TILES, HIDDEN], BF16)
-        ones = keep.tile([P, P], BF16)
         identity = keep.tile([P, P], F32)
         identity_bf = keep.tile([P, P], BF16)
         table_warm = keep.tile([P, 1], F32)
 
-        for gate in bias_rows:
-            nc.vector.memset(bias_rows[gate][:].bitcast(I32), 0)
-        nc.vector.memset(ones[:], 1.0)
-        for gate in GATES:
-            for src in SOURCES:
-                nc.vector.memset(w_planes[(gate, src)][:].rearrange("p g n -> p (g n)").bitcast(I32), 0)
-        nc.vector.memset(bias_square[:].bitcast(I32), 0)
+        def clear_planes(gate, src, engine):
+            engine.memset(w_planes[(gate, src)][:].rearrange("p g n -> p (g n)").bitcast(I32), 0)
+
         nc.vector.memset(table_warm[:], 0.0)
         nc.scalar.activation(out=table_warm[:], in_=table_warm[:], func=ACT.Sigmoid)
+        nc.vector.memset(bias_rows[:].bitcast(I32), 0)
+        clear_planes("f", "h", nc.vector)
+        clear_planes("f", "x", nc.vector)
+        nc.vector.memset(bias_square[:].bitcast(I32), 0)
         make_identity(nc, identity[:])
         nc.vector.tensor_copy(out=identity_bf[:], in_=identity[:])
 
         def load_bias_row(gate):
-            nc.sync.dma_start(out=bias_rows[gate][0:1, :], in_=dram_bias[gate].unsqueeze(0))
+            n = GATES.index(gate)
+            nc.sync.dma_start(out=bias_rows[n : n + 1, :], in_=dram_bias[gate].unsqueeze(0))
 
         def load_bias_column(gate):
             if True:
@@ -150,14 +148,20 @@ def tile_lstmcell_kernel(
             )
 
         load_scales("f", "h", nc.gpsimd, F32)
+        for src in SOURCES:
+            clear_planes("i", src, nc.gpsimd)
         for gate in ("i", "c"):
             load_bias_column(gate)
+        for gate in ("c", "o"):
+            for src in SOURCES:
+                clear_planes(gate, src, nc.gpsimd)
 
-        load_activation("x", 0, 2)
+        load_activation("x", 0, 1)
         load_bias_row("f")
         load_bias_row("i")
         load_bias_row("c")
         load_bias_row("o")
+        load_activation("x", 1, 1)
         load_activation("x", 2, 2)
         load_activation("h", 0, 2)
         load_activation("h", 2, 2)
@@ -215,12 +219,12 @@ def tile_lstmcell_kernel(
 
         def spread_bias(gate):
             spread = psum.tile([P, HIDDEN], BF16, name="spread", tag="bank")
+            n = GATES.index(gate)
+            picked = identity_bf[:, n : n + 1].to_broadcast([P, P])
             halves = [half for half in range(COL_HALVES) if (gate, half) in ROW_BANKS]
             for half in halves:
                 cols = slice(half * N_TILE, (half + 1) * N_TILE)
-                nc.tensor.matmul(
-                    out=spread[:, cols], lhsT=ones[:], rhs=bias_rows[gate][:, cols], start=True, stop=True
-                )
+                nc.tensor.matmul(out=spread[:, cols], lhsT=picked, rhs=bias_rows[:, cols], start=True, stop=True)
             used = slice(0, len(halves) * N_TILE)
             nc.scalar.copy(out=bias_all[gate][:, used], in_=spread[:, used])
 
@@ -399,9 +403,9 @@ def tile_lstmcell_kernel(
                         later.append((step + 1, lambda half=half, m=m: input_product(half, m, nc.vector)))
                         later.append((step + 2, lambda half=half, m=m: finish_cell(half, m)))
                     if gate == "o" and step < 31:
-                        later.append((step + (half == 0 and 0 or 1), lambda half=half, m=m: finish_hidden(half, m, nc.gpsimd if half == 0 else nc.vector)))
+                        later.append((step + (half == 0 and m < 3 and 0 or 2), lambda half=half, m=m: finish_hidden(half, m, nc.gpsimd if half == 0 and m < 3 else nc.vector)))
                     if step == 31:
-                        later.append((step + 2, lambda: finish_hidden(1, 3, nc.vector, 0, N_TILE // 2)))
-                        later.append((step + 2, lambda: finish_hidden(1, 3, nc.vector, N_TILE // 2, N_TILE // 2)))
+                        later.append((step + 3, lambda: finish_hidden(1, 3, nc.vector, 0, N_TILE // 2)))
+                        later.append((step + 3, lambda: finish_hidden(1, 3, nc.vector, N_TILE // 2, N_TILE // 2)))
                     emit(step)
         emit(1000)

@@ -98,19 +98,24 @@ def tile_lstmcell_kernel(
         c_sb = keep.tile([P, ROW_TILES, HIDDEN], BF16)
         identity = keep.tile([P, P], F32)
         identity_bf = keep.tile([P, P], BF16)
+        pick_row = keep.tile([P, len(GATES), P], BF16)
         table_warm = keep.tile([P, 1], F32)
 
-        def clear_planes(gate, src, engine):
-            engine.memset(w_planes[(gate, src)][:].rearrange("p g n -> p (g n)").bitcast(I32), 0)
+        def clear_planes(gate, src):
+            nc.vector.memset(w_planes[(gate, src)][:].rearrange("p g n -> p (g n)").bitcast(I32), 0)
 
         nc.vector.memset(table_warm[:], 0.0)
         nc.scalar.activation(out=table_warm[:], in_=table_warm[:], func=ACT.Sigmoid)
         nc.vector.memset(bias_rows[:].bitcast(I32), 0)
-        clear_planes("f", "h", nc.vector)
-        clear_planes("f", "x", nc.vector)
-        nc.vector.memset(bias_square[:].bitcast(I32), 0)
+        clear_planes("f", "h")
+        clear_planes("f", "x")
         make_identity(nc, identity[:])
         nc.vector.tensor_copy(out=identity_bf[:], in_=identity[:])
+        for n in range(len(GATES)):
+            nc.vector.tensor_copy(out=pick_row[:, n, :], in_=identity_bf[:, n : n + 1].to_broadcast([P, P]))
+        nc.vector.memset(bias_square[:].bitcast(I32), 0)
+        for src in SOURCES:
+            clear_planes("i", src)
 
         def load_bias_row(gate):
             n = GATES.index(gate)
@@ -148,20 +153,14 @@ def tile_lstmcell_kernel(
             )
 
         load_scales("f", "h", nc.gpsimd, F32)
-        for src in SOURCES:
-            clear_planes("i", src, nc.gpsimd)
         for gate in ("i", "c"):
             load_bias_column(gate)
-        for gate in ("c", "o"):
-            for src in SOURCES:
-                clear_planes(gate, src, nc.gpsimd)
 
-        load_activation("x", 0, 1)
+        load_activation("x", 0, 2)
         load_bias_row("f")
         load_bias_row("i")
         load_bias_row("c")
         load_bias_row("o")
-        load_activation("x", 1, 1)
         load_activation("x", 2, 2)
         load_activation("h", 0, 2)
         load_activation("h", 2, 2)
@@ -177,18 +176,6 @@ def tile_lstmcell_kernel(
         load_words("i", "h", 0)
         load_words("i", "h", 1)
         load_cell()
-        load_scales("c", "x")
-        load_words("c", "x", 0)
-        load_words("c", "x", 1)
-        load_scales("c", "h")
-        load_words("c", "h", 0)
-        load_words("c", "h", 1)
-        load_scales("o", "x")
-        load_words("o", "x", 0)
-        load_words("o", "x", 1)
-        load_scales("o", "h")
-        load_words("o", "h", 0)
-        load_words("o", "h", 1)
 
         def transpose_and_regroup(src, m):
             words = raw[src][:, m, :].bitcast(F32)
@@ -220,11 +207,10 @@ def tile_lstmcell_kernel(
         def spread_bias(gate):
             spread = psum.tile([P, HIDDEN], BF16, name="spread", tag="bank")
             n = GATES.index(gate)
-            picked = identity_bf[:, n : n + 1].to_broadcast([P, P])
             halves = [half for half in range(COL_HALVES) if (gate, half) in ROW_BANKS]
             for half in halves:
                 cols = slice(half * N_TILE, (half + 1) * N_TILE)
-                nc.tensor.matmul(out=spread[:, cols], lhsT=picked, rhs=bias_rows[:, cols], start=True, stop=True)
+                nc.tensor.matmul(out=spread[:, cols], lhsT=pick_row[:, n, :], rhs=bias_rows[:, cols], start=True, stop=True)
             used = slice(0, len(halves) * N_TILE)
             nc.scalar.copy(out=bias_all[gate][:, used], in_=spread[:, used])
 
@@ -243,6 +229,14 @@ def tile_lstmcell_kernel(
                 if m == 0 and src == "h":
                     quantise("x", 2, 2)
         quantise("h", 2, 2)
+        for gate in ("c", "o"):
+            for src in SOURCES:
+                clear_planes(gate, src)
+        for gate in ("c", "o"):
+            for src in SOURCES:
+                load_scales(gate, src)
+                for g in range(K_GROUPS):
+                    load_words(gate, src, g)
 
         passes = [(SOURCES.index(src), src, g) for src in SOURCES for g in range(K_GROUPS)]
         value = {}

from contextlib import ExitStack

import concourse.mybir as mybir
from concourse.masks import make_identity

F32 = mybir.dt.float32
BF16 = mybir.dt.bfloat16
I32 = mybir.dt.int32
U32 = mybir.dt.uint32
U8 = mybir.dt.uint8
FP8X4 = mybir.dt.float8_e4m3fn_x4
ACT = mybir.ActivationFunctionType
ALU = mybir.AluOpType

P = 128
BATCH = 512
FEATURES = 1024
HIDDEN = 1024
PACK = 4
K_PASS = P * PACK
K_GROUPS = FEATURES // K_PASS
ROW_TILES = BATCH // P
N_TILE = 512
COL_HALVES = HIDDEN // N_TILE
D_TILES = N_TILE // P
QUADRANTS = 4
SOURCES = ("x", "h")
GATES = ("f", "i", "c", "o")
ROW_BANKS = (("f", 0), ("f", 1), ("i", 0), ("c", 0), ("o", 0), ("o", 1))
GATE_BUFS = {"f": 8, "i": 8, "c": 6, "o": 8}

HEAD_BIASES = {("x", 0): "f", ("x", 1): "i", ("x", 3): "c", ("h", 1): "o"}

FLOPS = 2 * BATCH * (2 * FEATURES) * (4 * HIDDEN)


def tile_lstmcell_kernel(
    tc,
    x, h, c,
    W_xi_words, W_xi_scales, W_hi_words, W_hi_scales,
    W_xf_words, W_xf_scales, W_hf_words, W_hf_scales,
    W_xo_words, W_xo_scales, W_ho_words, W_ho_scales,
    W_xc_words, W_xc_scales, W_hc_words, W_hc_scales,
    b_i, b_f, b_o, b_c,
    out_0, out_1,
):
    nc = tc.nc
    activations = {"x": x, "h": h}
    dram_words = {
        ("i", "x"): W_xi_words, ("i", "h"): W_hi_words,
        ("f", "x"): W_xf_words, ("f", "h"): W_hf_words,
        ("o", "x"): W_xo_words, ("o", "h"): W_ho_words,
        ("c", "x"): W_xc_words, ("c", "h"): W_hc_words,
    }
    dram_scales = {
        ("i", "x"): W_xi_scales, ("i", "h"): W_hi_scales,
        ("f", "x"): W_xf_scales, ("f", "h"): W_hf_scales,
        ("o", "x"): W_xo_scales, ("o", "h"): W_ho_scales,
        ("c", "x"): W_xc_scales, ("c", "h"): W_hc_scales,
    }
    dram_bias = {"i": b_i, "f": b_f, "o": b_o, "c": b_c}

    with ExitStack() as stack:
        keep = stack.enter_context(tc.tile_pool(name="keep", bufs=1))
        work = stack.enter_context(tc.tile_pool(name="work", bufs=6))
        psum = stack.enter_context(tc.psum_pool(name="psum", bufs=8))
        stack.enter_context(tc.manual_schedule())

        raw = {}
        grouped = {}
        act_codes = {}
        act_scales = {}
        for src in SOURCES:
            raw[src] = keep.tile([P, ROW_TILES, FEATURES], BF16, name="raw_" + src)
            grouped[src] = keep.tile(
                [P, K_GROUPS, BATCH * PACK], BF16, name="grouped_" + src, align_bytes=64
            )
            act_codes[src] = keep.tile([P, K_GROUPS, BATCH], U32, name="codes_" + src, align_bytes=64)
            act_scales[src] = keep.tile([P, K_GROUPS, BATCH], U8, name="scales_" + src, align_bytes=64)
        w_words = {}
        for gate in GATES:
            for src in SOURCES:
                w_words[(gate, src)] = keep.tile(
                    [P, K_GROUPS, HIDDEN], U32, name="w_" + src + gate, align_bytes=64
                )
        w_planes = {}
        for gate in GATES:
            for src in SOURCES:
                w_planes[(gate, src)] = keep.tile(
                    [P, K_GROUPS, HIDDEN], U8, name="planes_" + src + gate, align_bytes=64
                )
        bias_rows = keep.tile([P, HIDDEN], BF16)
        bias_all = {}
        for gate in GATES:
            bias_all[gate] = keep.tile([P, HIDDEN], BF16, name="bias_all_" + gate)
        bias_square = keep.tile([P, P], BF16, name="bias_square")
        bias_cols = keep.tile([P, P], F32, name="bias_cols")
        c_sb = keep.tile([P, ROW_TILES, HIDDEN], BF16)
        identity = keep.tile([P, P], F32)
        identity_bf = keep.tile([P, P], BF16)
        pick_row = keep.tile([P, len(GATES), P], BF16)
        table_warm = keep.tile([P, 1], F32)

        def clear_planes(gate, src):
            nc.vector.memset(w_planes[(gate, src)][:].rearrange("p g n -> p (g n)").bitcast(I32), 0)

        nc.vector.memset(table_warm[:], 0.0)
        nc.scalar.activation(out=table_warm[:], in_=table_warm[:], func=ACT.Sigmoid)
        nc.vector.memset(bias_rows[:].bitcast(I32), 0)
        clear_planes("f", "h")
        clear_planes("f", "x")
        make_identity(nc, identity[:])
        nc.vector.tensor_copy(out=identity_bf[:], in_=identity[:])
        for n in range(len(GATES)):
            nc.vector.tensor_copy(out=pick_row[:, n, :], in_=identity_bf[:, n : n + 1].to_broadcast([P, P]))
        nc.vector.memset(bias_square[:].bitcast(I32), 0)
        for src in SOURCES:
            clear_planes("i", src)

        def load_bias_row(gate):
            n = GATES.index(gate)
            nc.sync.dma_start(out=bias_rows[n : n + 1, :], in_=dram_bias[gate].unsqueeze(0))

        def load_bias_column(gate):
            if True:
                first = (HIDDEN // P) * GATES.index(gate)
                nc.gpsimd.dma_start(
                    out=bias_square[first : first + HIDDEN // P, :],
                    in_=dram_bias[gate].rearrange("(j p) -> j p", p=P),
                )

        def load_scales(gate, src, queue=nc.sync, word=I32):
            for quad in range(QUADRANTS):
                queue.dma_start(
                    out=w_planes[(gate, src)][32 * quad : 32 * quad + 4, :, :].bitcast(word),
                    in_=dram_scales[(gate, src)].rearrange("g q n -> q g n")[4 * quad : 4 * quad + 4, :, :].bitcast(word),
                )

        def load_words(gate, src, g):
            words = dram_words[(gate, src)].rearrange("g p n t -> g p (n t)").bitcast(I32)
            nc.sync.dma_start(out=w_words[(gate, src)][:, g, :].bitcast(I32), in_=words[g])

        def load_activation(src, first, count):
            by_partition = activations[src].rearrange("(p m) k -> p (m k)", m=ROW_TILES)
            tiles = slice(first * FEATURES, (first + count) * FEATURES)
            side_by_side = raw[src][:].rearrange("p m k -> p (m k)")
            nc.sync.dma_start(out=side_by_side[:, tiles], in_=by_partition[:, tiles])

        def load_cell():
            nc.sync.dma_start(
                out=c_sb[:].rearrange("p m d -> p (m d)"),
                in_=c.rearrange("(p m) d -> p (m d)", m=ROW_TILES),
            )

        load_scales("f", "h", nc.gpsimd, F32)
        for gate in ("i", "c"):
            load_bias_column(gate)

        load_activation("x", 0, 2)
        load_bias_row("f")
        load_bias_row("i")
        load_bias_row("c")
        load_bias_row("o")
        load_activation("x", 2, 2)
        load_activation("h", 0, 2)
        load_activation("h", 2, 2)
        load_scales("f", "x")
        load_words("f", "x", 0)
        load_words("f", "x", 1)
        load_words("f", "h", 0)
        load_words("f", "h", 1)
        load_scales("i", "x")
        load_words("i", "x", 0)
        load_words("i", "x", 1)
        load_scales("i", "h")
        load_words("i", "h", 0)
        load_words("i", "h", 1)
        load_cell()

        def transpose_and_regroup(src, m):
            words = raw[src][:, m, :].bitcast(F32)
            flipped = psum.tile([P, K_GROUPS * 2, P], F32, name="flipped", tag="bank")
            for g in range(K_GROUPS):
                for u in range(2):
                    nc.tensor.transpose(
                        out=flipped[:, 2 * g + u, :],
                        in_=words[:, g * (K_PASS // 2) + u : (g + 1) * (K_PASS // 2) : 2],
                        identity=identity[:],
                    )
            side_by_side = grouped[src][:].bitcast(F32).rearrange("p g (b u) -> p g b u", u=2)
            side_by_side = side_by_side[:, :, m * P : (m + 1) * P, :]
            permuted = flipped[:].rearrange("p (g u) b -> p g b u", u=2)
            if m % 2 == 0:
                nc.vector.tensor_copy(out=side_by_side, in_=permuted)
            else:
                nc.scalar.copy(out=side_by_side, in_=permuted)

        def quantise(src, first_tile, tiles):
            rows = slice(first_tile * P, (first_tile + tiles) * P)
            for g in range(K_GROUPS):
                nc.vector.quantize_mx(
                    out=act_codes[src][:, g, rows].bitcast(FP8X4),
                    scales=act_scales[src][:, g, rows],
                    in_=grouped[src][:, g, first_tile * P * PACK : (first_tile + tiles) * P * PACK],
                )

        def spread_bias(gate):
            spread = psum.tile([P, HIDDEN], BF16, name="spread", tag="bank")
            n = GATES.index(gate)
            halves = [half for half in range(COL_HALVES) if (gate, half) in ROW_BANKS]
            for half in halves:
                cols = slice(half * N_TILE, (half + 1) * N_TILE)
                nc.tensor.matmul(out=spread[:, cols], lhsT=pick_row[:, n, :], rhs=bias_rows[:, cols], start=True, stop=True)
            used = slice(0, len(halves) * N_TILE)
            nc.scalar.copy(out=bias_all[gate][:, used], in_=spread[:, used])

        def turn_bias_square():
            turned = psum.tile([P, P], BF16, name="turned", tag="bank")
            nc.tensor.transpose(out=turned[:], in_=bias_square[:], identity=identity_bf[:])
            nc.scalar.copy(out=bias_cols[:], in_=turned[:])

        for src in SOURCES:
            for m in range(ROW_TILES):
                transpose_and_regroup(src, m)
                if (src, m) in HEAD_BIASES:
                    spread_bias(HEAD_BIASES[(src, m)])
                if m == 2:
                    quantise(src, 0, 2)
                if m == 0 and src == "h":
                    quantise("x", 2, 2)
        quantise("h", 2, 2)
        for gate in ("c", "o"):
            for src in SOURCES:
                clear_planes(gate, src)
        for gate in ("c", "o"):
            for src in SOURCES:
                load_scales(gate, src)
                for g in range(K_GROUPS):
                    load_words(gate, src, g)

        passes = [(SOURCES.index(src), src, g) for src in SOURCES for g in range(K_GROUPS)]
        value = {}
        product_bank = {}

        def row_passes(acc, gate, half, m, chosen, first=0, width=N_TILE):
            rows = slice(m * P, (m + 1) * P)
            cols = slice(half * N_TILE + first, half * N_TILE + first + width)
            for s, src, g in chosen:
                n = K_GROUPS * s + g
                nc.tensor.matmul_mx(
                    out=acc[:],
                    lhsT=act_codes[src][:, g, rows].bitcast(FP8X4),
                    lhsT_scale=act_scales[src][:, g, rows],
                    rhs=w_words[(gate, src)][:, g, cols].bitcast(FP8X4),
                    rhs_scale=w_planes[(gate, src)][:, g, cols],
                    start=(n == 0),
                    stop=(n == len(passes) - 1),
                )

        def col_passes(acc, gate, d_tile):
            channels = slice(d_tile * P, (d_tile + 1) * P)
            for s, src, g in passes:
                n = K_GROUPS * s + g
                nc.tensor.matmul_mx(
                    out=acc[:],
                    lhsT=w_words[(gate, src)][:, g, channels].bitcast(FP8X4),
                    lhsT_scale=w_planes[(gate, src)][:, g, channels],
                    rhs=act_codes[src][:, g, :].bitcast(FP8X4),
                    rhs_scale=act_scales[src][:, g, :],
                    start=(n == 0),
                    stop=(n == len(passes) - 1),
                )

        def finish_row_bank(acc, gate, half, m, first=0, width=N_TILE):
            cols = slice(half * N_TILE + first, half * N_TILE + first + width)
            if first == 0:
                value[(gate, half, m)] = work.tile(
                    [P, N_TILE], F32, name="gate_" + gate, tag="gate_" + gate, bufs=GATE_BUFS[gate]
                )
            part = value[(gate, half, m)][:, first : first + width]
            nc.vector.tensor_tensor(out=part, in0=acc[:], in1=bias_all[gate][:, cols], op=ALU.add)
            nc.scalar.activation(out=part, in_=part, func=(ACT.Tanh if gate == "c" else ACT.Sigmoid))

        def row_bank(gate, half, m, first=0, width=N_TILE):
            acc = psum.tile([P, width], F32, name="acc", tag="bank")
            row_passes(acc, gate, half, m, passes, first, width)
            finish_row_bank(acc, gate, half, m, first, width)

        def col_bank(gate, half, j):
            d_tile = half * D_TILES + j
            acc = psum.tile([P, N_TILE], F32, name="acc", tag="bank")
            col_passes(acc, gate, d_tile)
            gate_sb = work.tile([P, N_TILE], F32, name="gate_" + gate, tag="gate_" + gate, bufs=GATE_BUFS[gate])
            value[(gate, half, j)] = gate_sb
            column = (HIDDEN // P) * GATES.index(gate) + d_tile
            nc.scalar.activation(
                out=gate_sb[:],
                in_=acc[:],
                func=(ACT.Tanh if gate == "c" else ACT.Sigmoid),
                bias=bias_cols[:, column : column + 1],
            )

        def times_c(half, m, engine):
            forget = value[("f", half, m)]
            cols = slice(half * N_TILE, (half + 1) * N_TILE)
            engine.tensor_tensor(out=forget[:], in0=forget[:], in1=c_sb[:, m, cols], op=ALU.mult)

        def input_product(half, j, engine):
            candidate = value[("c", half, j)]
            engine.tensor_tensor(
                out=candidate[:], in0=value[("i", half, j)][:], in1=candidate[:], op=ALU.mult
            )

        def turn_products(half):
            for m in range(ROW_TILES):
                bank = psum.tile([P, D_TILES, P], F32, name="products", tag="bank")
                product_bank[m] = bank
                for j in range(D_TILES):
                    nc.tensor.transpose(
                        out=bank[:, j, :],
                        in_=value[("c", half, j)][:, m * P : (m + 1) * P],
                        identity=identity[:],
                    )

        def by_row_tile(out):
            return out.rearrange("(p m) d -> p m d", m=ROW_TILES)

        def finish_cell(half, m):
            cell = value[("f", half, m)]
            if ("c", half) in ROW_BANKS:
                products = value[("c", half, m)][:]
            else:
                products = product_bank[m][:].rearrange("p j d -> p (j d)")
            nc.vector.tensor_tensor(out=cell[:], in0=products, in1=cell[:], op=ALU.add)
            nc.sync.dma_start(
                out=by_row_tile(out_1)[:, m, half * N_TILE : (half + 1) * N_TILE], in_=cell[:]
            )
            cell_tanh = work.tile([P, N_TILE], F32, name="cell_tanh", tag="cell_tanh")
            value[("t", half, m)] = cell_tanh
            nc.scalar.activation(out=cell_tanh[:], in_=cell[:], func=ACT.Tanh)

        def finish_hidden(half, m, engine, first=0, width=N_TILE):
            part = slice(first, first + width)
            cols = slice(half * N_TILE + first, half * N_TILE + first + width)
            hidden = value[("o", half, m)]
            engine.tensor_tensor(
                out=hidden[:, part], in0=hidden[:, part], in1=value[("t", half, m)][:, part], op=ALU.mult
            )
            nc.sync.dma_start(out=by_row_tile(out_0)[:, m, cols], in_=hidden[:, part])

        first_banks = {}
        for half in range(COL_HALVES):
            for m in range(ROW_TILES):
                first_banks[(half, m)] = psum.tile([P, N_TILE], F32, name="acc_first", tag="bank")
                row_passes(first_banks[(half, m)], "f", half, m, passes[:1])
        for chosen in passes[1:-1]:
            for half in range(COL_HALVES):
                for m in range(ROW_TILES):
                    row_passes(first_banks[(half, m)], "f", half, m, [chosen])
        later = []

        def emit(now):
            for due in sorted(set(d for d, w in later if d <= now)):
                for d, w in [x for x in later if x[0] == due]:
                    w()
            later[:] = [x for x in later if x[0] > now]

        n = 0
        for gate, half in (("f", 0), ("f", 1), ("i", 0), ("i", 1), ("c", 0), ("c", 1), ("o", 0), ("o", 1)):
            for m in range(ROW_TILES):
                if True:
                    step = n
                    n += 1
                    emit(step - 0.5)
                    if gate == "f":
                        row_passes(first_banks[(half, m)], "f", half, m, passes[-1:])
                        finish_row_bank(first_banks[(half, m)], "f", half, m)
                    elif step == 4 * ROW_TILES * COL_HALVES - 1:
                        piece = N_TILE // 2
                        row_bank("o", 1, 3, 0, piece)
                        row_bank("o", 1, 3, piece, piece)
                    elif (gate, half) in ROW_BANKS:
                        row_bank(gate, half, m)
                    else:
                        col_bank(gate, half, m)
                    if step == 11:
                        turn_bias_square()
                    if gate == ("i"):
                        later.append((step + 0, lambda half=half, m=m: times_c(half, m, nc.vector)))
                    if gate == "c" and (gate, half) not in ROW_BANKS:
                        later.append((step + 0.5, lambda half=half, m=m: input_product(half, m, nc.vector)))
                        if m == 3:
                            later.append((step + 3, lambda half=half: turn_products(half)))
                            for mm, lag in enumerate((3, 3, 3, 4)):
                                later.append((step + lag, lambda half=half, mm=mm: finish_cell(half, mm)))
                    if gate == "c" and (gate, half) in ROW_BANKS:
                        later.append((step + 1, lambda half=half, m=m: input_product(half, m, nc.vector)))
                        later.append((step + 2, lambda half=half, m=m: finish_cell(half, m)))
                    if gate == "o" and step < 31:
                        later.append((step + (half == 0 and m < 3 and 0 or 2), lambda half=half, m=m: finish_hidden(half, m, nc.gpsimd if half == 0 and m < 3 else nc.vector)))
                    if step == 31:
                        later.append((step + 3, lambda: finish_hidden(1, 3, nc.vector, 0, N_TILE // 2)))
                        later.append((step + 3, lambda: finish_hidden(1, 3, nc.vector, N_TILE // 2, N_TILE // 2)))
                    emit(step)
        emit(1000)
